import numpy as np
import ml_dtypes


def mxq(x, axis, fmt="e4m3"):
    dtype, down = {"e4m3": (ml_dtypes.float8_e4m3fn, 7), "e5m2": (ml_dtypes.float8_e5m2, 14)}[fmt]
    v = np.moveaxis(np.asarray(x, np.float32).astype(ml_dtypes.bfloat16).astype(np.float64), axis, -1)
    blocks = v.reshape(v.shape[:-1] + (-1, 32))
    amax = np.abs(blocks).max(-1, keepdims=True)
    byte = np.maximum(np.where(amax > 0, np.frexp(amax)[1] - 1 + 127, 0) - down, 1)
    scale = np.exp2(byte - 127.0)
    codes = (blocks / scale).astype(np.float32).astype(dtype).astype(np.float64)
    return np.moveaxis((codes * scale).reshape(v.shape), -1, axis)


WIDE = False


def mx_kscale(k):
    if not WIDE:
        return np.ones(k)
    levels = np.array([10, -10, 5, -5, 0])
    if k % 512:
        return np.exp2(np.random.permutation(np.resize(levels, k // 32))).repeat(32)
    a = np.empty((k // 512, 16))
    for p in range(k // 512):
        a[p, :8] = np.random.permutation(np.resize(levels, 8))
        for g in range(8):
            far = levels[np.abs(levels - a[p, g]) >= 10]
            a[p, g + 8] = far[np.random.randint(len(far))]
    return np.exp2(a.ravel()).repeat(32)


BF16 = ml_dtypes.bfloat16


def bf(x):
    return np.asarray(x, np.float32).astype(BF16)


def f64(x):
    return np.asarray(x).astype(np.float64)


N, DIN, DOUT = 1024, 1024, 1024
EPS = 1e-7


def artanh(v):
    return 0.5 * np.log((1.0 + v) / (1.0 - v))


def logmap0(p):
    n = np.sqrt(np.sum(p * p, axis=-1, keepdims=True))
    n_safe = np.clip(n, EPS, 1.0 - EPS)
    return artanh(n_safe) * p / n_safe


def expmap0(v):
    n = np.sqrt(np.sum(v * v, axis=-1, keepdims=True))
    n_safe = np.maximum(n, EPS)
    return np.tanh(n_safe) * v / n_safe


def setup_inputs():
    s = mx_kscale(DIN)
    c = np.sqrt(np.mean(s * s))
    g = np.random.standard_normal((N, DIN)) * s
    rad = 0.1 + 0.4 * np.random.random((N, 1))
    mid = rad * g / np.sqrt(np.sum(g * g, axis=1, keepdims=True))
    return {"mid": bf(mid),
            "W": bf(np.random.standard_normal((DIN, DOUT)) * 4.0 / np.sqrt(DOUT) * c / s[:, None]),
            "b": bf(np.random.standard_normal(DOUT) * 0.7 / np.sqrt(DOUT))}


def reference(mid, W, b):
    u = logmap0(f64(mid))
    y = np.maximum((mxq(u, 1, "e4m3") @ mxq(f64(W), 0, "e4m3")) + f64(b), 0.0)
    return expmap0(y)

@@ -1,0 +1,284 @@
+from contextlib import ExitStack
+
+import concourse.mybir as mybir
+from concourse.masks import make_identity
+
+FLOPS = 2 * 1024 * 1024 * 1024
+
+F32 = mybir.dt.float32
+BF16 = mybir.dt.bfloat16
+U32 = mybir.dt.uint32
+U8 = mybir.dt.uint8
+FP8X4 = mybir.dt.float8_e4m3fn_x4
+ALU = mybir.AluOpType
+ACT = mybir.ActivationFunctionType
+
+P = 128
+SIZE = 1024
+ROW_TILES = SIZE // P
+PACK = 4
+PAIRS = 2
+K_PASS = P * PACK
+PASSES = SIZE // K_PASS
+BANK = 512
+HALVES = SIZE // BANK
+BATCH = 4
+EPS = 1e-7
+PIECES = [(0, 0), (1, 0), (0, 1), (1, 1)]
+
+
+def tile_graphconvhyp_pb_kernel(tc, mid, W, b, out):
+    nc = tc.nc
+    with ExitStack() as ctx:
+        const = ctx.enter_context(tc.tile_pool(name="const", bufs=1))
+        rows_in = ctx.enter_context(tc.tile_pool(name="rows_in", bufs=ROW_TILES))
+        w_in = ctx.enter_context(tc.tile_pool(name="w_in", bufs=len(PIECES)))
+        w_grouped = ctx.enter_context(tc.tile_pool(name="w_grouped", bufs=len(PIECES)))
+        u_rows = ctx.enter_context(tc.tile_pool(name="u_rows", bufs=ROW_TILES))
+        u_grouped = ctx.enter_context(tc.tile_pool(name="u_grouped", bufs=ROW_TILES))
+        unread = ctx.enter_context(tc.tile_pool(name="unread", bufs=2))
+        y_rows = ctx.enter_context(tc.tile_pool(name="y_rows", bufs=ROW_TILES))
+        stats = ctx.enter_context(tc.tile_pool(name="stats", bufs=ROW_TILES))
+        ps_t = ctx.enter_context(tc.psum_pool(name="ps_t", bufs=4))
+        ps_y = ctx.enter_context(tc.psum_pool(name="ps_y", bufs=4))
+
+        ident = const.tile([P, P], F32, name="ident")
+        ones = const.tile([P, P], BF16, name="ones")
+        b_row = const.tile([P, SIZE], BF16, name="b_row")
+        b_all = const.tile([P, SIZE], BF16, name="b_all")
+        one = const.tile([P, 1], F32, name="one")
+        warm = const.tile([P, 1], F32, name="warm")
+        plus_minus = const.tile([P, 2], F32, name="plus_minus")
+        half = const.tile([P, BATCH], F32, name="half")
+        minus_half = const.tile([P, 1], F32, name="minus_half")
+        w_codes = const.tile([P, PASSES, SIZE], U32, name="w_codes", align_bytes=64)
+        w_scales = const.tile([P, PASSES, SIZE], U8, name="w_scales", align_bytes=64)
+        u_codes = const.tile([P, ROW_TILES, PASSES * P], U32, name="u_codes", align_bytes=64)
+        u_scales = const.tile([P, ROW_TILES, PASSES * P], U8, name="u_scales", align_bytes=64)
+
+        mid_t = {}
+        w_raw = {}
+        w_grp = {}
+        n_sq, n_clip, norm, inv_norm, logs, factor = {}, {}, {}, {}, {}, {}
+        u_t, u_ps, u_grp = {}, {}, {}
+        b_ps, y_ps = {}, {}
+        y_t, m_sq, inv_m, gain = {}, {}, {}, {}
+
+        def load_rows(i):
+            mid_t[i] = rows_in.tile([P, SIZE], BF16, name="mid_t")
+            nc.sync.dma_start(out=mid_t[i][:], in_=mid[i * P:(i + 1) * P, :])
+
+        def load_w(q):
+            g, h = PIECES[q]
+            w_raw[q] = w_in.tile([P, PACK, BANK], BF16, name="w_raw")
+            nc.sync.dma_start(
+                out=w_raw[q][:],
+                in_=W[g * K_PASS:(g + 1) * K_PASS, h * BANK:(h + 1) * BANK].rearrange(
+                    "(p t) n -> p t n", t=PACK, p=P
+                ),
+            )
+
+        def regroup_w(q):
+            w_grp[q] = w_grouped.tile([P, BANK, PACK], BF16, name="w_grp", align_bytes=64)
+            nc.vector.tensor_copy(
+                out=w_grp[q][:].rearrange("p (c i) t -> p c t i", i=4),
+                in_=w_raw[q][:].rearrange("p t (c i) -> p c t i", i=4),
+            )
+
+        def quantise_w(q):
+            g, h = PIECES[q]
+            nc.vector.quantize_mx(
+                out=w_codes[:, g, h * BANK:(h + 1) * BANK].bitcast(FP8X4),
+                scales=w_scales[:, g, h * BANK:(h + 1) * BANK],
+                in_=w_grp[q][:].rearrange("p n t -> p (n t)"),
+            )
+
+        def square_sum(i):
+            bt, c = divmod(i, BATCH)
+            if c == 0:
+                n_sq[bt] = stats.tile([P, BATCH], F32, name="n_sq")
+            squares = unread.tile([P, SIZE], BF16, name="squares")
+            nc.scalar.activation(out=squares[:], in_=mid_t[i][:], func=ACT.Square,
+                                 accum_out=n_sq[bt][:, c:c + 1])
+
+        def norm_root(bt):
+            n_clip[bt] = stats.tile([P, BATCH], F32, name="n_clip")
+            norm[bt] = stats.tile([P, BATCH], F32, name="norm")
+            nc.gpsimd.tensor_scalar(out=n_clip[bt][:], in0=n_sq[bt][:],
+                                    scalar1=(1.0 - EPS) * (1.0 - EPS), scalar2=EPS * EPS,
+                                    op0=ALU.min, op1=ALU.max)
+            nc.gpsimd.tensor_tensor(out=norm[bt][:], in0=n_clip[bt][:], in1=half[:], op=ALU.pow)
+
+        def norm_recip(bt):
+            inv_norm[bt] = stats.tile([P, BATCH], F32, name="inv_norm")
+            nc.vector.reciprocal(out=inv_norm[bt][:], in_=norm[bt][:])
+
+        def log_terms(i):
+            bt, c = divmod(i, BATCH)
+            if c == 0:
+                logs[bt] = stats.tile([P, BATCH, 2], F32, name="logs")
+            nc.scalar.activation(out=logs[bt][:, c, :], in_=plus_minus[:], func=ACT.Ln,
+                                 scale=norm[bt][:, c:c + 1], bias=one[:, 0:1])
+
+        def scale_factor(bt):
+            diff = stats.tile([P, BATCH], F32, name="diff")
+            factor[bt] = stats.tile([P, BATCH], F32, name="factor")
+            nc.vector.tensor_tensor(out=diff[:], in0=logs[bt][:, :, 0], in1=logs[bt][:, :, 1],
+                                    op=ALU.subtract)
+            nc.vector.tensor_tensor(out=factor[bt][:], in0=diff[:], in1=inv_norm[bt][:],
+                                    op=ALU.mult)
+
+        def scale_rows(i):
+            bt, c = divmod(i, BATCH)
+            u_t[i] = u_rows.tile([P, SIZE], BF16, name="u_t")
+            nc.vector.tensor_scalar(out=u_t[i][:], in0=mid_t[i][:],
+                                    scalar1=factor[bt][:, c:c + 1], scalar2=0.5,
+                                    op0=ALU.mult, op1=ALU.mult)
+
+        def transpose_rows(i):
+            u_ps[i] = ps_t.tile([P, PASSES, PAIRS, P], F32, name="u_ps")
+            words = u_t[i][:].bitcast(F32)
+            for g in range(PASSES):
+                for e in range(PAIRS):
+                    first = g * P * PAIRS + e
+                    nc.tensor.transpose(u_ps[i][:, g, e, :],
+                                        words[:, first:(g + 1) * P * PAIRS:PAIRS], ident[:])
+
+        def regroup_rows(i):
+            u_grp[i] = u_grouped.tile([P, PASSES, P, PAIRS], F32, name="u_grp", align_bytes=64)
+            nc.scalar.copy(out=u_grp[i][:], in_=u_ps[i][:].rearrange("p g e r -> p g r e"))
+
+        def quantise_rows(i):
+            nc.vector.quantize_mx(
+                out=u_codes[:, i, :].bitcast(FP8X4),
+                scales=u_scales[:, i, :],
+                in_=u_grp[i][:].rearrange("p g r e -> p (g r e)").bitcast(BF16),
+            )
+
+        def multiply(i):
+            for h in range(HALVES):
+                y_ps[i, h] = ps_y.tile([P, BANK], F32, name="y_ps", tag="y_ps")
+                for g in range(PASSES):
+                    nc.tensor.matmul_mx(
+                        out=y_ps[i, h][:],
+                        lhsT=u_codes[:, i, g * P:(g + 1) * P].bitcast(FP8X4),
+                        lhsT_scale=u_scales[:, i, g * P:(g + 1) * P],
+                        rhs=w_codes[:, g, h * BANK:(h + 1) * BANK].bitcast(FP8X4),
+                        rhs_scale=w_scales[:, g, h * BANK:(h + 1) * BANK],
+                        start=(g == 0),
+                        stop=(g == PASSES - 1),
+                    )
+
+        def add_bias(i):
+            y_t[i] = y_rows.tile([P, SIZE], F32, name="y_t")
+            for h in range(HALVES):
+                nc.vector.tensor_tensor(out=y_t[i][:, h * BANK:(h + 1) * BANK], in0=y_ps[i, h][:],
+                                        in1=b_all[:, h * BANK:(h + 1) * BANK], op=ALU.add)
+
+        def sum_squares(i):
+            products = unread.tile([P, SIZE], F32, name="products")
+            total = stats.tile([P, 1], F32, name="total")
+            m_sq[i] = stats.tile([P, 1], F32, name="m_sq")
+            nc.vector.scalar_tensor_tensor(out=products[:], in0=y_t[i][:], scalar=0.0,
+                                           in1=y_t[i][:], op0=ALU.max, op1=ALU.mult,
+                                           accum_out=total[:])
+            nc.vector.tensor_scalar(out=m_sq[i][:], in0=total[:], scalar1=EPS * EPS, scalar2=None,
+                                    op0=ALU.max)
+
+        def norm2_root(i):
+            inv_m[i] = stats.tile([P, 1], F32, name="inv_m")
+            nc.gpsimd.tensor_tensor(out=inv_m[i][:], in0=m_sq[i][:], in1=minus_half[:], op=ALU.pow)
+
+        def out_gain(i):
+            tanh_m = stats.tile([P, 1], F32, name="tanh_m")
+            gain[i] = stats.tile([P, 1], F32, name="gain")
+            nc.scalar.activation(out=tanh_m[:], in_=m_sq[i][:], func=ACT.Tanh, scale=inv_m[i][:, 0:1])
+            nc.scalar.activation(out=gain[i][:], in_=tanh_m[:], func=ACT.Copy, scale=inv_m[i][:, 0:1])
+
+        def scale_out(i):
+            if i == ROW_TILES - 1:
+                nc.vector.tensor_scalar(out=y_t[i][:], in0=y_t[i][:], scalar1=0.0,
+                                        scalar2=gain[i][:, 0:1], op0=ALU.max, op1=ALU.mult)
+            else:
+                nc.scalar.activation(out=y_t[i][:], in_=y_t[i][:], func=ACT.Relu,
+                                     scale=gain[i][:, 0:1])
+            nc.sync.dma_start(out=out[i * P:(i + 1) * P, :], in_=y_t[i][:])
+
+        nc.vector.memset(one[:], 1.0)
+        nc.vector.memset(b_row[:], 0.0)
+        nc.vector.memset(ones[:], 1.0)
+        nc.gpsimd.memset(half[:], 0.5)
+        nc.gpsimd.memset(minus_half[:], -0.5)
+        nc.gpsimd.memset(plus_minus[:, 0:1], 1.0)
+        nc.gpsimd.memset(plus_minus[:, 1:2], -1.0)
+        make_identity(nc, ident[:])
+        nc.scalar.dma_start(out=b_row[0:1, :], in_=b.rearrange("(o n) -> o n", o=1))
+        nc.scalar.activation(out=warm[:], in_=one[:], func=ACT.Ln)
+
+        load_rows(0)
+        for q in range(len(PIECES)):
+            load_rows(q + 1)
+            load_w(q)
+        for i in range(len(PIECES) + 1, ROW_TILES):
+            load_rows(i)
+
+        for h in range(HALVES):
+            b_ps[h] = ps_y.tile([P, BANK], F32, name="b_ps", tag="y_ps")
+            nc.tensor.matmul(out=b_ps[h][:], lhsT=ones[:], rhs=b_row[:, h * BANK:(h + 1) * BANK],
+                             start=True, stop=True)
+
+        for i in range(BATCH):
+            square_sum(i)
+        regroup_w(0)
+        regroup_w(1)
+        quantise_w(0)
+        norm_root(0)
+        for h in range(HALVES):
+            nc.vector.tensor_copy(out=b_all[:, h * BANK:(h + 1) * BANK], in_=b_ps[h][:])
+        norm_recip(0)
+        square_sum(BATCH)
+        for i in range(BATCH):
+            log_terms(i)
+        for i in range(BATCH + 1, ROW_TILES):
+            square_sum(i)
+        norm_root(1)
+        regroup_w(2)
+        quantise_w(1)
+        scale_factor(0)
+        for i in (0, 1):
+            scale_rows(i)
+            transpose_rows(i)
+        quantise_w(2)
+        regroup_w(3)
+        for i in (2, 3):
+            scale_rows(i)
+            transpose_rows(i)
+        regroup_rows(0)
+        quantise_rows(0)
+        quantise_w(3)
+        regroup_rows(1)
+        quantise_rows(1)
+        regroup_rows(2)
+        for i in range(BATCH, ROW_TILES):
+            log_terms(i)
+        regroup_rows(3)
+        multiply(0)
+        multiply(1)
+
+        for i in range(ROW_TILES):
+            add_bias(i)
+            if i == 1:
+                norm_recip(1)
+                scale_factor(1)
+                for later in range(BATCH, ROW_TILES):
+                    scale_rows(later)
+            if 1 <= i <= BATCH:
+                transpose_rows(i + BATCH - 1)
+                regroup_rows(i + BATCH - 1)
+            sum_squares(i)
+            norm2_root(i)
+            if i + 2 < ROW_TILES:
+                quantise_rows(i + 2)
+                multiply(i + 2)
+            out_gain(i)
+            scale_out(i)

@@ -22,9 +22,12 @@ K_PASS = P * PACK
 PASSES = SIZE // K_PASS
 BANK = 512
 HALVES = SIZE // BANK
-BATCH = 4
 EPS = 1e-7
 PIECES = [(0, 0), (1, 0), (0, 1), (1, 1)]
+BATCHES = [(0, 1), (2, 3, 4), (5, 6, 7)]
+LAST = ROW_TILES - 1
+SPLITS = (192, 192, 192, 192, 256, 256, 256, 384)
+VECTOR_NORMS = (0,)
 
 
 def tile_graphconvhyp_pb_kernel(tc, mid, W, b, out):
@@ -39,30 +42,27 @@ def tile_graphconvhyp_pb_kernel(tc, mid, W, b, out):
         unread = ctx.enter_context(tc.tile_pool(name="unread", bufs=2))
         y_rows = ctx.enter_context(tc.tile_pool(name="y_rows", bufs=ROW_TILES))
         stats = ctx.enter_context(tc.tile_pool(name="stats", bufs=ROW_TILES))
-        ps_t = ctx.enter_context(tc.psum_pool(name="ps_t", bufs=4))
-        ps_y = ctx.enter_context(tc.psum_pool(name="ps_y", bufs=4))
+        ps_t = ctx.enter_context(tc.psum_pool(name="ps_t", bufs=3))
+        ps_y = ctx.enter_context(tc.psum_pool(name="ps_y", bufs=5))
 
         ident = const.tile([P, P], F32, name="ident")
         ones = const.tile([P, P], BF16, name="ones")
         b_row = const.tile([P, SIZE], BF16, name="b_row")
         b_all = const.tile([P, SIZE], BF16, name="b_all")
         one = const.tile([P, 1], F32, name="one")
-        warm = const.tile([P, 1], F32, name="warm")
-        plus_minus = const.tile([P, 2], F32, name="plus_minus")
-        half = const.tile([P, BATCH], F32, name="half")
-        minus_half = const.tile([P, 1], F32, name="minus_half")
+        warm = const.tile([P, 2], F32, name="warm")
+        half = const.tile([P, ROW_TILES], F32, name="half")
+        minus_half = const.tile([P, ROW_TILES], F32, name="minus_half")
         w_codes = const.tile([P, PASSES, SIZE], U32, name="w_codes", align_bytes=64)
         w_scales = const.tile([P, PASSES, SIZE], U8, name="w_scales", align_bytes=64)
         u_codes = const.tile([P, ROW_TILES, PASSES * P], U32, name="u_codes", align_bytes=64)
         u_scales = const.tile([P, ROW_TILES, PASSES * P], U8, name="u_scales", align_bytes=64)
 
-        mid_t = {}
-        w_raw = {}
-        w_grp = {}
-        n_sq, n_clip, norm, inv_norm, logs, factor = {}, {}, {}, {}, {}, {}
-        u_t, u_ps, u_grp = {}, {}, {}
-        b_ps, y_ps = {}, {}
-        y_t, m_sq, inv_m, gain = {}, {}, {}, {}
+        mid_t, w_raw, w_grp = {}, {}, {}
+        n_sq, norm, half_inv, log_ratio = {}, {}, {}, {}
+        u_t, u_ps, u_grp, y_ps, y_t = {}, {}, {}, {}, {}
+        totals, m_sq, inv_m, tanh_m, gain = {}, {}, {}, {}, {}
+        place = {i: (bt, c) for bt, batch in enumerate(BATCHES) for c, i in enumerate(batch)}
 
         def load_rows(i):
             mid_t[i] = rows_in.tile([P, SIZE], BF16, name="mid_t")
@@ -77,6 +77,14 @@ def tile_graphconvhyp_pb_kernel(tc, mid, W, b, out):
                     "(p t) n -> p t n", t=PACK, p=P
                 ),
             )
+
+        def spread_b():
+            b_ps = ps_y.tile([P, SIZE], BF16, name="b_ps", tag="y_ps")
+            for h in range(HALVES):
+                cols = slice(h * BANK, (h + 1) * BANK)
+                nc.tensor.matmul(out=b_ps[:, cols], lhsT=ones[:], rhs=b_row[:, cols],
+                                 start=True, stop=True)
+            nc.vector.tensor_copy(out=b_all[:], in_=b_ps[:])
 
         def regroup_w(q):
             w_grp[q] = w_grouped.tile([P, BANK, PACK], BF16, name="w_grp", align_bytes=64)
@@ -94,46 +102,45 @@ def tile_graphconvhyp_pb_kernel(tc, mid, W, b, out):
             )
 
         def square_sum(i):
-            bt, c = divmod(i, BATCH)
+            bt, c = place[i]
             if c == 0:
-                n_sq[bt] = stats.tile([P, BATCH], F32, name="n_sq")
-            squares = unread.tile([P, SIZE], BF16, name="squares")
-            nc.scalar.activation(out=squares[:], in_=mid_t[i][:], func=ACT.Square,
-                                 accum_out=n_sq[bt][:, c:c + 1])
+                n_sq[bt] = stats.tile([P, len(BATCHES[bt])], F32, name="n_sq", tag="n_sq%d" % bt, bufs=1)
+            if i in VECTOR_NORMS:
+                v_squares = unread.tile([P, SIZE], BF16, name="v_squares")
+                nc.vector.scalar_tensor_tensor(out=v_squares[:], in0=mid_t[i][:], scalar=1.0, in1=mid_t[i][:],
+                                               op0=ALU.mult, op1=ALU.mult, accum_out=n_sq[bt][:, c:c + 1])
+            else:
+                squares = unread.tile([P, SIZE], BF16, name="squares")
+                nc.scalar.activation(out=squares[:], in_=mid_t[i][:], func=ACT.Square,
+                                     accum_out=n_sq[bt][:, c:c + 1])
 
         def norm_root(bt):
-            n_clip[bt] = stats.tile([P, BATCH], F32, name="n_clip")
-            norm[bt] = stats.tile([P, BATCH], F32, name="norm")
-            nc.gpsimd.tensor_scalar(out=n_clip[bt][:], in0=n_sq[bt][:],
+            w = len(BATCHES[bt])
+            n_clip = stats.tile([P, w], F32, name="n_clip", tag="n_clip%d" % bt, bufs=1)
+            norm[bt] = stats.tile([P, w], F32, name="norm", tag="norm%d" % bt, bufs=1)
+            four_sq = stats.tile([P, w], F32, name="four_sq", tag="four_sq%d" % bt, bufs=1)
+            half_inv[bt] = stats.tile([P, w], F32, name="half_inv", tag="half_inv%d" % bt, bufs=1)
+            nc.gpsimd.tensor_scalar(out=n_clip[:], in0=n_sq[bt][:],
                                     scalar1=(1.0 - EPS) * (1.0 - EPS), scalar2=EPS * EPS,
                                     op0=ALU.min, op1=ALU.max)
-            nc.gpsimd.tensor_tensor(out=norm[bt][:], in0=n_clip[bt][:], in1=half[:], op=ALU.pow)
+            nc.gpsimd.tensor_tensor(out=norm[bt][:], in0=n_clip[:], in1=half[:, :w], op=ALU.pow)
+            nc.gpsimd.tensor_scalar(out=four_sq[:], in0=n_clip[:], scalar1=4.0, scalar2=0.0, op0=ALU.mult, op1=ALU.add)
+            nc.gpsimd.tensor_tensor(out=half_inv[bt][:], in0=four_sq[:], in1=minus_half[:, :w], op=ALU.pow)
 
-        def norm_recip(bt):
-            inv_norm[bt] = stats.tile([P, BATCH], F32, name="inv_norm")
-            nc.vector.reciprocal(out=inv_norm[bt][:], in_=norm[bt][:])
-
-        def log_terms(i):
-            bt, c = divmod(i, BATCH)
-            if c == 0:
-                logs[bt] = stats.tile([P, BATCH, 2], F32, name="logs")
-            nc.scalar.activation(out=logs[bt][:, c, :], in_=plus_minus[:], func=ACT.Ln,
-                                 scale=norm[bt][:, c:c + 1], bias=one[:, 0:1])
-
-        def scale_factor(bt):
-            diff = stats.tile([P, BATCH], F32, name="diff")
-            factor[bt] = stats.tile([P, BATCH], F32, name="factor")
-            nc.vector.tensor_tensor(out=diff[:], in0=logs[bt][:, :, 0], in1=logs[bt][:, :, 1],
-                                    op=ALU.subtract)
-            nc.vector.tensor_tensor(out=factor[bt][:], in0=diff[:], in1=inv_norm[bt][:],
-                                    op=ALU.mult)
+        def log_terms(bt):
+            w = len(BATCHES[bt])
+            ln_plus = stats.tile([P, w], F32, name="ln_plus", tag="ln_plus%d" % bt, bufs=1)
+            ln_minus = stats.tile([P, w], F32, name="ln_minus", tag="ln_minus%d" % bt, bufs=1)
+            log_ratio[bt] = stats.tile([P, w], F32, name="log_ratio", tag="log_ratio%d" % bt, bufs=1)
+            nc.scalar.activation(out=ln_plus[:], in_=norm[bt][:], func=ACT.Ln, scale=1.0, bias=one[:, 0:1])
+            nc.scalar.activation(out=ln_minus[:], in_=norm[bt][:], func=ACT.Ln, scale=-1.0, bias=one[:, 0:1])
+            nc.gpsimd.tensor_tensor(out=log_ratio[bt][:], in0=ln_plus[:], in1=ln_minus[:], op=ALU.subtract)
 
         def scale_rows(i):
-            bt, c = divmod(i, BATCH)
+            bt, c = place[i]
             u_t[i] = u_rows.tile([P, SIZE], BF16, name="u_t")
-            nc.vector.tensor_scalar(out=u_t[i][:], in0=mid_t[i][:],
-                                    scalar1=factor[bt][:, c:c + 1], scalar2=0.5,
-                                    op0=ALU.mult, op1=ALU.mult)
+            nc.vector.tensor_scalar(out=u_t[i][:], in0=mid_t[i][:], scalar1=log_ratio[bt][:, c:c + 1],
+                                    scalar2=half_inv[bt][:, c:c + 1], op0=ALU.mult, op1=ALU.mult)
 
         def transpose_rows(i):
             u_ps[i] = ps_t.tile([P, PASSES, PAIRS, P], F32, name="u_ps")
@@ -155,130 +162,149 @@ def tile_graphconvhyp_pb_kernel(tc, mid, W, b, out):
                 in_=u_grp[i][:].rearrange("p g r e -> p (g r e)").bitcast(BF16),
             )
 
-        def multiply(i):
-            for h in range(HALVES):
-                y_ps[i, h] = ps_y.tile([P, BANK], F32, name="y_ps", tag="y_ps")
-                for g in range(PASSES):
-                    nc.tensor.matmul_mx(
-                        out=y_ps[i, h][:],
-                        lhsT=u_codes[:, i, g * P:(g + 1) * P].bitcast(FP8X4),
-                        lhsT_scale=u_scales[:, i, g * P:(g + 1) * P],
-                        rhs=w_codes[:, g, h * BANK:(h + 1) * BANK].bitcast(FP8X4),
-                        rhs_scale=w_scales[:, g, h * BANK:(h + 1) * BANK],
-                        start=(g == 0),
-                        stop=(g == PASSES - 1),
-                    )
+        def multiply(i, h):
+            y_ps[i, h] = ps_y.tile([P, BANK], F32, name="y_ps", tag="y_ps")
+            for g in range(PASSES):
+                nc.tensor.matmul_mx(
+                    out=y_ps[i, h][:],
+                    lhsT=u_codes[:, i, g * P:(g + 1) * P].bitcast(FP8X4),
+                    lhsT_scale=u_scales[:, i, g * P:(g + 1) * P],
+                    rhs=w_codes[:, g, h * BANK:(h + 1) * BANK].bitcast(FP8X4),
+                    rhs_scale=w_scales[:, g, h * BANK:(h + 1) * BANK],
+                    start=(g == 0),
+                    stop=(g == PASSES - 1),
+                )
 
-        def add_bias(i):
-            y_t[i] = y_rows.tile([P, SIZE], F32, name="y_t")
-            for h in range(HALVES):
-                nc.vector.tensor_tensor(out=y_t[i][:, h * BANK:(h + 1) * BANK], in0=y_ps[i, h][:],
-                                        in1=b_all[:, h * BANK:(h + 1) * BANK], op=ALU.add)
+        def add_bias(i, h):
+            if h == 0:
+                y_t[i] = y_rows.tile([P, SIZE], F32, name="y_t")
+            cols = slice(h * BANK, (h + 1) * BANK)
+            nc.vector.tensor_tensor(out=y_t[i][:, cols], in0=y_ps[i, h][:], in1=b_all[:, cols], op=ALU.add)
 
-        def sum_squares(i):
-            products = unread.tile([P, SIZE], F32, name="products")
-            total = stats.tile([P, 1], F32, name="total")
-            m_sq[i] = stats.tile([P, 1], F32, name="m_sq")
-            nc.vector.scalar_tensor_tensor(out=products[:], in0=y_t[i][:], scalar=0.0,
-                                           in1=y_t[i][:], op0=ALU.max, op1=ALU.mult,
-                                           accum_out=total[:])
-            nc.vector.tensor_scalar(out=m_sq[i][:], in0=total[:], scalar1=EPS * EPS, scalar2=None,
-                                    op0=ALU.max)
+        def scalar_relu(i):
+            y = y_t[i][:, :SPLITS[i]]
+            nc.scalar.activation(out=y, in_=y, func=ACT.Relu)
+
+        def scalar_squares(i):
+            totals[i] = stats.tile([P, 2], F32, name="total")
+            squares = unread.tile([P, SIZE], F32, name="s_squares")
+            nc.scalar.activation(out=squares[:, :SPLITS[i]], in_=y_t[i][:, :SPLITS[i]], func=ACT.Square,
+                                 accum_out=totals[i][:, 0:1])
+
+        def vector_squares(i):
+            y = y_t[i][:, SPLITS[i]:]
+            squares = unread.tile([P, SIZE], F32, name="v_products")
+            nc.vector.scalar_tensor_tensor(out=squares[:, SPLITS[i]:], in0=y, scalar=0.0, in1=y,
+                                           op0=ALU.max, op1=ALU.mult, accum_out=totals[i][:, 1:2])
 
         def norm2_root(i):
+            m_sq[i] = stats.tile([P, 1], F32, name="m_sq")
             inv_m[i] = stats.tile([P, 1], F32, name="inv_m")
-            nc.gpsimd.tensor_tensor(out=inv_m[i][:], in0=m_sq[i][:], in1=minus_half[:], op=ALU.pow)
+            nc.gpsimd.tensor_scalar(out=m_sq[i][:], in0=totals[i][:, 0:1], scalar1=totals[i][:, 1:2],
+                                    scalar2=EPS * EPS, op0=ALU.add, op1=ALU.max)
+            nc.gpsimd.tensor_tensor(out=inv_m[i][:], in0=m_sq[i][:], in1=minus_half[:, 0:1], op=ALU.pow)
+
+        def out_tanh(i):
+            tanh_m[i] = stats.tile([P, 1], F32, name="tanh_m")
+            nc.scalar.activation(out=tanh_m[i][:], in_=m_sq[i][:], func=ACT.Tanh, scale=inv_m[i][:, 0:1])
 
         def out_gain(i):
-            tanh_m = stats.tile([P, 1], F32, name="tanh_m")
             gain[i] = stats.tile([P, 1], F32, name="gain")
-            nc.scalar.activation(out=tanh_m[:], in_=m_sq[i][:], func=ACT.Tanh, scale=inv_m[i][:, 0:1])
-            nc.scalar.activation(out=gain[i][:], in_=tanh_m[:], func=ACT.Copy, scale=inv_m[i][:, 0:1])
+            nc.scalar.activation(out=gain[i][:], in_=tanh_m[i][:], func=ACT.Copy, scale=inv_m[i][:, 0:1])
 
-        def scale_out(i):
-            if i == ROW_TILES - 1:
-                nc.vector.tensor_scalar(out=y_t[i][:], in0=y_t[i][:], scalar1=0.0,
-                                        scalar2=gain[i][:, 0:1], op0=ALU.max, op1=ALU.mult)
-            else:
-                nc.scalar.activation(out=y_t[i][:], in_=y_t[i][:], func=ACT.Relu,
-                                     scale=gain[i][:, 0:1])
-            nc.sync.dma_start(out=out[i * P:(i + 1) * P, :], in_=y_t[i][:])
+        def scale_on_vector(i, cols):
+            nc.vector.tensor_scalar(out=y_t[i][:, cols], in0=y_t[i][:, cols], scalar1=0.0,
+                                    scalar2=gain[i][:, 0:1], op0=ALU.max, op1=ALU.mult)
 
-        nc.vector.memset(one[:], 1.0)
+        def scale_on_scalar(i, cols):
+            nc.scalar.activation(out=y_t[i][:, cols], in_=y_t[i][:, cols], func=ACT.Relu,
+                                 scale=gain[i][:, 0:1])
+
+        def store(i, cols):
+            nc.sync.dma_start(out=out[i * P:(i + 1) * P, cols], in_=y_t[i][:, cols])
+
+        ctx.enter_context(tc.manual_schedule())
         nc.vector.memset(b_row[:], 0.0)
+        nc.vector.memset(one[:], 1.0)
         nc.vector.memset(ones[:], 1.0)
         nc.gpsimd.memset(half[:], 0.5)
         nc.gpsimd.memset(minus_half[:], -0.5)
-        nc.gpsimd.memset(plus_minus[:, 0:1], 1.0)
-        nc.gpsimd.memset(plus_minus[:, 1:2], -1.0)
         make_identity(nc, ident[:])
-        nc.scalar.dma_start(out=b_row[0:1, :], in_=b.rearrange("(o n) -> o n", o=1))
-        nc.scalar.activation(out=warm[:], in_=one[:], func=ACT.Ln)
-
+        nc.scalar.activation(out=warm[:, 0:1], in_=one[:], func=ACT.Ln)
         load_rows(0)
-        for q in range(len(PIECES)):
-            load_rows(q + 1)
-            load_w(q)
-        for i in range(len(PIECES) + 1, ROW_TILES):
-            load_rows(i)
+        nc.sync.dma_start(out=b_row[0:1, :], in_=b.rearrange("(o n) -> o n", o=1))
+        for load, which in ((load_rows, 1), (load_w, 0), (load_rows, 2), (load_w, 1), (load_rows, 3),
+                            (load_rows, 4), (load_w, 2), (load_w, 3), (load_rows, 5), (load_rows, 6), (load_rows, 7)):
+            load(which)
 
-        for h in range(HALVES):
-            b_ps[h] = ps_y.tile([P, BANK], F32, name="b_ps", tag="y_ps")
-            nc.tensor.matmul(out=b_ps[h][:], lhsT=ones[:], rhs=b_row[:, h * BANK:(h + 1) * BANK],
-                             start=True, stop=True)
-
-        for i in range(BATCH):
-            square_sum(i)
+        square_sum(0)
+        square_sum(1)
+        spread_b()
+        norm_root(0)
         regroup_w(0)
+        square_sum(2)
+        log_terms(0)
         regroup_w(1)
         quantise_w(0)
-        norm_root(0)
-        for h in range(HALVES):
-            nc.vector.tensor_copy(out=b_all[:, h * BANK:(h + 1) * BANK], in_=b_ps[h][:])
-        norm_recip(0)
-        square_sum(BATCH)
-        for i in range(BATCH):
-            log_terms(i)
-        for i in range(BATCH + 1, ROW_TILES):
-            square_sum(i)
-        norm_root(1)
-        regroup_w(2)
-        quantise_w(1)
-        scale_factor(0)
+        square_sum(3)
         for i in (0, 1):
             scale_rows(i)
             transpose_rows(i)
-        quantise_w(2)
+        quantise_w(1)
+        square_sum(4)
+        norm_root(1)
+        regroup_w(2)
+        regroup_rows(0)
+        quantise_rows(0)
+        multiply(0, 0)
+        log_terms(1)
+        square_sum(5)
         regroup_w(3)
+        regroup_rows(1)
+        quantise_w(2)
+        quantise_rows(1)
+        quantise_w(3)
+        multiply(0, 1)
+        square_sum(6)
         for i in (2, 3):
             scale_rows(i)
             transpose_rows(i)
-        regroup_rows(0)
-        quantise_rows(0)
-        quantise_w(3)
-        regroup_rows(1)
-        quantise_rows(1)
+        multiply(1, 0)
+        multiply(1, 1)
+        square_sum(7)
+        norm_root(2)
         regroup_rows(2)
-        for i in range(BATCH, ROW_TILES):
-            log_terms(i)
         regroup_rows(3)
-        multiply(0)
-        multiply(1)
+        log_terms(2)
+        nc.scalar.activation(out=warm[:, 1:2], in_=one[:], func=ACT.Tanh)
 
-        for i in range(ROW_TILES):
-            add_bias(i)
-            if i == 1:
-                norm_recip(1)
-                scale_factor(1)
-                for later in range(BATCH, ROW_TILES):
-                    scale_rows(later)
-            if 1 <= i <= BATCH:
-                transpose_rows(i + BATCH - 1)
-                regroup_rows(i + BATCH - 1)
-            sum_squares(i)
-            norm2_root(i)
-            if i + 2 < ROW_TILES:
-                quantise_rows(i + 2)
-                multiply(i + 2)
-            out_gain(i)
-            scale_out(i)
+        whole = slice(0, SIZE)
+        for r in range(ROW_TILES):
+            add_bias(r, 0)
+            if r + 4 < ROW_TILES:
+                scale_rows(r + 4)
+                transpose_rows(r + 4)
+            add_bias(r, 1)
+            scalar_relu(r)
+            if r > 0:
+                out_tanh(r - 1)
+            scalar_squares(r)
+            if r > 0:
+                out_gain(r - 1)
+            if r + 4 < ROW_TILES:
+                regroup_rows(r + 4)
+            if r > 0:
+                scale_on_scalar(r - 1, whole)
+                store(r - 1, whole)
+            if r + 2 < ROW_TILES:
+                quantise_rows(r + 2)
+                multiply(r + 2, 0)
+                multiply(r + 2, 1)
+            vector_squares(r)
+            norm2_root(r)
+        out_tanh(LAST)
+        out_gain(LAST)
+        scale_on_scalar(LAST, slice(0, BANK))
+        store(LAST, slice(0, BANK))
+        scale_on_vector(LAST, slice(BANK, SIZE))
+        store(LAST, slice(BANK, SIZE))

@@ -24,10 +24,14 @@ BANK = 512
 HALVES = SIZE // BANK
 EPS = 1e-7
 PIECES = [(0, 0), (1, 0), (0, 1), (1, 1)]
-BATCHES = [(0, 1), (2, 3, 4), (5, 6, 7)]
+BATCHES = [(0, 1, 2, 3, 4, 5, 6, 7)]
 LAST = ROW_TILES - 1
+TAIL = 384
+SCALAR_W = (1,)
 SPLITS = (192, 192, 192, 192, 256, 256, 256, 384)
-VECTOR_NORMS = (0,)
+VECTOR_NORMS = (0, 2, 4, 6)
+VECTOR_REGROUPS = ()
+VECTOR_OUTS = ()
 
 
 def tile_graphconvhyp_pb_kernel(tc, mid, W, b, out):
@@ -58,8 +62,8 @@ def tile_graphconvhyp_pb_kernel(tc, mid, W, b, out):
         u_codes = const.tile([P, ROW_TILES, PASSES * P], U32, name="u_codes", align_bytes=64)
         u_scales = const.tile([P, ROW_TILES, PASSES * P], U8, name="u_scales", align_bytes=64)
 
-        mid_t, w_raw, w_grp = {}, {}, {}
-        n_sq, norm, half_inv, log_ratio = {}, {}, {}, {}
+        mid_t, w_raw, w_grp, b_ps = {}, {}, {}, {}
+        n_sq, n_raw, norm, half_inv, logs, ratio = {}, {}, {}, {}, {}, {}
         u_t, u_ps, u_grp, y_ps, y_t = {}, {}, {}, {}, {}
         totals, m_sq, inv_m, tanh_m, gain = {}, {}, {}, {}, {}
         place = {i: (bt, c) for bt, batch in enumerate(BATCHES) for c, i in enumerate(batch)}
@@ -78,17 +82,20 @@ def tile_graphconvhyp_pb_kernel(tc, mid, W, b, out):
                 ),
             )
 
-        def spread_b():
-            b_ps = ps_y.tile([P, SIZE], BF16, name="b_ps", tag="y_ps")
+        def spread_ps():
+            b_ps["b"] = ps_y.tile([P, SIZE], BF16, name="b_ps", tag="y_ps")
             for h in range(HALVES):
                 cols = slice(h * BANK, (h + 1) * BANK)
-                nc.tensor.matmul(out=b_ps[:, cols], lhsT=ones[:], rhs=b_row[:, cols],
+                nc.tensor.matmul(out=b_ps["b"][:, cols], lhsT=ones[:], rhs=b_row[:, cols],
                                  start=True, stop=True)
-            nc.vector.tensor_copy(out=b_all[:], in_=b_ps[:])
+
+        def spread_copy():
+            nc.vector.tensor_copy(out=b_all[:], in_=b_ps["b"][:])
 
         def regroup_w(q):
             w_grp[q] = w_grouped.tile([P, BANK, PACK], BF16, name="w_grp", align_bytes=64)
-            nc.vector.tensor_copy(
+            copy = nc.scalar.copy if q in SCALAR_W else nc.vector.tensor_copy
+            copy(
                 out=w_grp[q][:].rearrange("p (c i) t -> p c t i", i=4),
                 in_=w_raw[q][:].rearrange("p t (c i) -> p c t i", i=4),
             )
@@ -105,41 +112,43 @@ def tile_graphconvhyp_pb_kernel(tc, mid, W, b, out):
             bt, c = place[i]
             if c == 0:
                 n_sq[bt] = stats.tile([P, len(BATCHES[bt])], F32, name="n_sq", tag="n_sq%d" % bt, bufs=1)
+            total = n_sq[bt][:, c:c + 1]
             if i in VECTOR_NORMS:
                 v_squares = unread.tile([P, SIZE], BF16, name="v_squares")
-                nc.vector.scalar_tensor_tensor(out=v_squares[:], in0=mid_t[i][:], scalar=1.0, in1=mid_t[i][:],
-                                               op0=ALU.mult, op1=ALU.mult, accum_out=n_sq[bt][:, c:c + 1])
+                nc.vector.scalar_tensor_tensor(out=v_squares[:], in0=mid_t[i][:], scalar=4.0, in1=mid_t[i][:],
+                                               op0=ALU.mult, op1=ALU.mult, accum_out=total)
             else:
-                squares = unread.tile([P, SIZE], BF16, name="squares")
-                nc.scalar.activation(out=squares[:], in_=mid_t[i][:], func=ACT.Square,
-                                     accum_out=n_sq[bt][:, c:c + 1])
+                s_squares = unread.tile([P, SIZE], BF16, name="s_squares")
+                nc.scalar.activation(out=s_squares[:], in_=mid_t[i][:], func=ACT.Square, scale=2.0, accum_out=total)
 
         def norm_root(bt):
             w = len(BATCHES[bt])
-            n_clip = stats.tile([P, w], F32, name="n_clip", tag="n_clip%d" % bt, bufs=1)
-            norm[bt] = stats.tile([P, w], F32, name="norm", tag="norm%d" % bt, bufs=1)
-            four_sq = stats.tile([P, w], F32, name="four_sq", tag="four_sq%d" % bt, bufs=1)
-            half_inv[bt] = stats.tile([P, w], F32, name="half_inv", tag="half_inv%d" % bt, bufs=1)
-            nc.gpsimd.tensor_scalar(out=n_clip[:], in0=n_sq[bt][:],
-                                    scalar1=(1.0 - EPS) * (1.0 - EPS), scalar2=EPS * EPS,
-                                    op0=ALU.min, op1=ALU.max)
-            nc.gpsimd.tensor_tensor(out=norm[bt][:], in0=n_clip[:], in1=half[:, :w], op=ALU.pow)
-            nc.gpsimd.tensor_scalar(out=four_sq[:], in0=n_clip[:], scalar1=4.0, scalar2=0.0, op0=ALU.mult, op1=ALU.add)
-            nc.gpsimd.tensor_tensor(out=half_inv[bt][:], in0=four_sq[:], in1=minus_half[:, :w], op=ALU.pow)
+            n_raw[bt] = stats.tile([P, w], F32, name="n_raw", tag="n_raw%d" % bt, bufs=1)
+            nc.gpsimd.tensor_tensor(out=n_raw[bt][:], in0=n_sq[bt][:], in1=half[:, :w], op=ALU.pow)
+
+        def norm_clip(bt):
+            norm[bt] = stats.tile([P, len(BATCHES[bt])], F32, name="norm", tag="norm%d" % bt, bufs=1)
+            nc.vector.tensor_scalar(out=norm[bt][:], in0=n_raw[bt][:], scalar1=2.0 * (1.0 - EPS),
+                                    scalar2=2.0 * EPS, op0=ALU.min, op1=ALU.max)
+
+        def norm_recip(bt):
+            half_inv[bt] = stats.tile([P, len(BATCHES[bt])], F32, name="half_inv", tag="half_inv%d" % bt, bufs=1)
+            nc.vector.reciprocal(out=half_inv[bt][:], in_=norm[bt][:])
 
         def log_terms(bt):
             w = len(BATCHES[bt])
-            ln_plus = stats.tile([P, w], F32, name="ln_plus", tag="ln_plus%d" % bt, bufs=1)
-            ln_minus = stats.tile([P, w], F32, name="ln_minus", tag="ln_minus%d" % bt, bufs=1)
-            log_ratio[bt] = stats.tile([P, w], F32, name="log_ratio", tag="log_ratio%d" % bt, bufs=1)
-            nc.scalar.activation(out=ln_plus[:], in_=norm[bt][:], func=ACT.Ln, scale=1.0, bias=one[:, 0:1])
-            nc.scalar.activation(out=ln_minus[:], in_=norm[bt][:], func=ACT.Ln, scale=-1.0, bias=one[:, 0:1])
-            nc.gpsimd.tensor_tensor(out=log_ratio[bt][:], in0=ln_plus[:], in1=ln_minus[:], op=ALU.subtract)
+            logs[bt] = stats.tile([P, 2, w], F32, name="logs", tag="logs%d" % bt, bufs=1)
+            nc.scalar.activation(out=logs[bt][:, 0, :], in_=norm[bt][:], func=ACT.Ln, scale=0.5, bias=one[:, 0:1])
+            nc.scalar.activation(out=logs[bt][:, 1, :], in_=norm[bt][:], func=ACT.Ln, scale=-0.5, bias=one[:, 0:1])
+
+        def log_ratios(bt):
+            ratio[bt] = stats.tile([P, len(BATCHES[bt])], F32, name="ratio", tag="ratio%d" % bt, bufs=1)
+            nc.vector.tensor_tensor(out=ratio[bt][:], in0=logs[bt][:, 0, :], in1=logs[bt][:, 1, :], op=ALU.subtract)
 
         def scale_rows(i):
             bt, c = place[i]
             u_t[i] = u_rows.tile([P, SIZE], BF16, name="u_t")
-            nc.vector.tensor_scalar(out=u_t[i][:], in0=mid_t[i][:], scalar1=log_ratio[bt][:, c:c + 1],
+            nc.vector.tensor_scalar(out=u_t[i][:], in0=mid_t[i][:], scalar1=ratio[bt][:, c:c + 1],
                                     scalar2=half_inv[bt][:, c:c + 1], op0=ALU.mult, op1=ALU.mult)
 
         def transpose_rows(i):
@@ -153,7 +162,10 @@ def tile_graphconvhyp_pb_kernel(tc, mid, W, b, out):
 
         def regroup_rows(i):
             u_grp[i] = u_grouped.tile([P, PASSES, P, PAIRS], F32, name="u_grp", align_bytes=64)
-            nc.scalar.copy(out=u_grp[i][:], in_=u_ps[i][:].rearrange("p g e r -> p g r e"))
+            if i in VECTOR_REGROUPS:
+                nc.vector.tensor_copy(out=u_grp[i][:], in_=u_ps[i][:].rearrange("p g e r -> p g r e"))
+            else:
+                nc.scalar.copy(out=u_grp[i][:], in_=u_ps[i][:].rearrange("p g e r -> p g r e"))
 
         def quantise_rows(i):
             nc.vector.quantize_mx(
@@ -186,22 +198,24 @@ def tile_graphconvhyp_pb_kernel(tc, mid, W, b, out):
             nc.scalar.activation(out=y, in_=y, func=ACT.Relu)
 
         def scalar_squares(i):
-            totals[i] = stats.tile([P, 2], F32, name="total")
-            squares = unread.tile([P, SIZE], F32, name="s_squares")
-            nc.scalar.activation(out=squares[:, :SPLITS[i]], in_=y_t[i][:, :SPLITS[i]], func=ACT.Square,
+            totals[i] = stats.tile([P, 2], F32, name="totals")
+            s_products = unread.tile([P, SIZE], F32, name="s_products")
+            nc.scalar.activation(out=s_products[:, :SPLITS[i]], in_=y_t[i][:, :SPLITS[i]], func=ACT.Square,
                                  accum_out=totals[i][:, 0:1])
 
         def vector_squares(i):
             y = y_t[i][:, SPLITS[i]:]
-            squares = unread.tile([P, SIZE], F32, name="v_products")
-            nc.vector.scalar_tensor_tensor(out=squares[:, SPLITS[i]:], in0=y, scalar=0.0, in1=y,
+            v_products = unread.tile([P, SIZE], F32, name="v_products")
+            nc.vector.scalar_tensor_tensor(out=v_products[:, SPLITS[i]:], in0=y, scalar=0.0, in1=y,
                                            op0=ALU.max, op1=ALU.mult, accum_out=totals[i][:, 1:2])
 
-        def norm2_root(i):
+        def norm2_floor(i):
             m_sq[i] = stats.tile([P, 1], F32, name="m_sq")
-            inv_m[i] = stats.tile([P, 1], F32, name="inv_m")
-            nc.gpsimd.tensor_scalar(out=m_sq[i][:], in0=totals[i][:, 0:1], scalar1=totals[i][:, 1:2],
+            nc.vector.tensor_scalar(out=m_sq[i][:], in0=totals[i][:, 0:1], scalar1=totals[i][:, 1:2],
                                     scalar2=EPS * EPS, op0=ALU.add, op1=ALU.max)
+
+        def norm2_root(i):
+            inv_m[i] = stats.tile([P, 1], F32, name="inv_m")
             nc.gpsimd.tensor_tensor(out=inv_m[i][:], in0=m_sq[i][:], in1=minus_half[:, 0:1], op=ALU.pow)
 
         def out_tanh(i):
@@ -223,6 +237,14 @@ def tile_graphconvhyp_pb_kernel(tc, mid, W, b, out):
         def store(i, cols):
             nc.sync.dma_start(out=out[i * P:(i + 1) * P, cols], in_=y_t[i][:, cols])
 
+        def scale_out(i):
+            whole = slice(0, SIZE)
+            if i in VECTOR_OUTS:
+                scale_on_vector(i, whole)
+            else:
+                scale_on_scalar(i, whole)
+            store(i, whole)
+
         ctx.enter_context(tc.manual_schedule())
         nc.vector.memset(b_row[:], 0.0)
         nc.vector.memset(one[:], 1.0)
@@ -233,78 +255,76 @@ def tile_graphconvhyp_pb_kernel(tc, mid, W, b, out):
         nc.scalar.activation(out=warm[:, 0:1], in_=one[:], func=ACT.Ln)
         load_rows(0)
         nc.sync.dma_start(out=b_row[0:1, :], in_=b.rearrange("(o n) -> o n", o=1))
-        for load, which in ((load_rows, 1), (load_w, 0), (load_rows, 2), (load_w, 1), (load_rows, 3),
-                            (load_rows, 4), (load_w, 2), (load_w, 3), (load_rows, 5), (load_rows, 6), (load_rows, 7)):
-            load(which)
+        for i in range(1, ROW_TILES):
+            load_rows(i)
+        for q in range(len(PIECES)):
+            load_w(q)
 
-        square_sum(0)
-        square_sum(1)
-        spread_b()
+        for i in range(ROW_TILES):
+            square_sum(i)
+        spread_ps()
         norm_root(0)
         regroup_w(0)
-        square_sum(2)
-        log_terms(0)
+        spread_copy()
         regroup_w(1)
         quantise_w(0)
-        square_sum(3)
+        norm_clip(0)
+        norm_recip(0)
+        log_terms(0)
+        nc.scalar.activation(out=warm[:, 1:2], in_=one[:], func=ACT.Tanh)
+        regroup_w(2)
+        log_ratios(0)
         for i in (0, 1):
             scale_rows(i)
             transpose_rows(i)
+            regroup_rows(i)
         quantise_w(1)
-        square_sum(4)
-        norm_root(1)
-        regroup_w(2)
-        regroup_rows(0)
-        quantise_rows(0)
-        multiply(0, 0)
-        log_terms(1)
-        square_sum(5)
         regroup_w(3)
-        regroup_rows(1)
-        quantise_w(2)
-        quantise_rows(1)
-        quantise_w(3)
-        multiply(0, 1)
-        square_sum(6)
         for i in (2, 3):
             scale_rows(i)
             transpose_rows(i)
+            regroup_rows(i)
+        quantise_w(2)
+        quantise_rows(0)
+        multiply(0, 0)
+        quantise_rows(1)
+        quantise_w(3)
+        multiply(0, 1)
         multiply(1, 0)
         multiply(1, 1)
-        square_sum(7)
-        norm_root(2)
-        regroup_rows(2)
-        regroup_rows(3)
-        log_terms(2)
-        nc.scalar.activation(out=warm[:, 1:2], in_=one[:], func=ACT.Tanh)
+        for i in range(4, 4):
+            scale_rows(i)
+            transpose_rows(i)
+            regroup_rows(i)
+        quantise_rows(2)
 
-        whole = slice(0, SIZE)
         for r in range(ROW_TILES):
             add_bias(r, 0)
-            if r + 4 < ROW_TILES:
+            add_bias(r, 1)
+            if 4 <= r + 4 < ROW_TILES:
                 scale_rows(r + 4)
                 transpose_rows(r + 4)
-            add_bias(r, 1)
             scalar_relu(r)
             if r > 0:
                 out_tanh(r - 1)
             scalar_squares(r)
             if r > 0:
                 out_gain(r - 1)
-            if r + 4 < ROW_TILES:
+            if 4 <= r + 4 < ROW_TILES:
                 regroup_rows(r + 4)
-            if r > 0:
-                scale_on_scalar(r - 1, whole)
-                store(r - 1, whole)
             if r + 2 < ROW_TILES:
-                quantise_rows(r + 2)
                 multiply(r + 2, 0)
                 multiply(r + 2, 1)
             vector_squares(r)
+            if r > 0:
+                scale_out(r - 1)
+            if r + 3 < ROW_TILES:
+                quantise_rows(r + 3)
+            norm2_floor(r)
             norm2_root(r)
         out_tanh(LAST)
         out_gain(LAST)
-        scale_on_scalar(LAST, slice(0, BANK))
-        store(LAST, slice(0, BANK))
-        scale_on_vector(LAST, slice(BANK, SIZE))
-        store(LAST, slice(BANK, SIZE))
+        scale_on_scalar(LAST, slice(0, TAIL))
+        store(LAST, slice(0, TAIL))
+        scale_on_vector(LAST, slice(TAIL, SIZE))
+        store(LAST, slice(TAIL, SIZE))

@@ -24,13 +24,14 @@ BANK = 512
 HALVES = SIZE // BANK
 EPS = 1e-7
 PIECES = [(0, 0), (1, 0), (0, 1), (1, 1)]
-BATCHES = [(0, 1, 2, 3, 4, 5, 6, 7)]
+BATCHES = [(0, 1), (2, 3, 4, 5), (6, 7)]
 LAST = ROW_TILES - 1
+SCALAR_W = (3,)
+SCALAR_SUMS = (0, 4)
 TAIL = 384
-SCALAR_W = (1,)
-SPLITS = (192, 192, 192, 192, 256, 256, 256, 384)
-VECTOR_NORMS = (0, 2, 4, 6)
-VECTOR_REGROUPS = ()
+EXTRA = 1
+VECTOR_NORMS = (0,)
+VECTOR_REGROUPS = (0, 1)
 VECTOR_OUTS = ()
 
 
@@ -44,7 +45,6 @@ def tile_graphconvhyp_pb_kernel(tc, mid, W, b, out):
         u_rows = ctx.enter_context(tc.tile_pool(name="u_rows", bufs=ROW_TILES))
         u_grouped = ctx.enter_context(tc.tile_pool(name="u_grouped", bufs=ROW_TILES))
         unread = ctx.enter_context(tc.tile_pool(name="unread", bufs=2))
-        y_rows = ctx.enter_context(tc.tile_pool(name="y_rows", bufs=ROW_TILES))
         stats = ctx.enter_context(tc.tile_pool(name="stats", bufs=ROW_TILES))
         ps_t = ctx.enter_context(tc.psum_pool(name="ps_t", bufs=3))
         ps_y = ctx.enter_context(tc.psum_pool(name="ps_y", bufs=5))
@@ -59,13 +59,14 @@ def tile_graphconvhyp_pb_kernel(tc, mid, W, b, out):
         minus_half = const.tile([P, ROW_TILES], F32, name="minus_half")
         w_codes = const.tile([P, PASSES, SIZE], U32, name="w_codes", align_bytes=64)
         w_scales = const.tile([P, PASSES, SIZE], U8, name="w_scales", align_bytes=64)
+        y_all = const.tile([P, ROW_TILES, SIZE + EXTRA], F32, name="y_all")
         u_codes = const.tile([P, ROW_TILES, PASSES * P], U32, name="u_codes", align_bytes=64)
         u_scales = const.tile([P, ROW_TILES, PASSES * P], U8, name="u_scales", align_bytes=64)
 
         mid_t, w_raw, w_grp, b_ps = {}, {}, {}, {}
         n_sq, n_raw, norm, half_inv, logs, ratio = {}, {}, {}, {}, {}, {}
-        u_t, u_ps, u_grp, y_ps, y_t = {}, {}, {}, {}, {}
-        totals, m_sq, inv_m, tanh_m, gain = {}, {}, {}, {}, {}
+        u_t, u_ps, u_grp, y_ps = {}, {}, {}, {}
+        m_sq, inv_m, tanh_m, gain = {}, {}, {}, {}
         place = {i: (bt, c) for bt, batch in enumerate(BATCHES) for c, i in enumerate(batch)}
 
         def load_rows(i):
@@ -188,31 +189,26 @@ def tile_graphconvhyp_pb_kernel(tc, mid, W, b, out):
                 )
 
         def add_bias(i, h):
-            if h == 0:
-                y_t[i] = y_rows.tile([P, SIZE], F32, name="y_t")
             cols = slice(h * BANK, (h + 1) * BANK)
-            nc.vector.tensor_tensor(out=y_t[i][:, cols], in0=y_ps[i, h][:], in1=b_all[:, cols], op=ALU.add)
+            nc.vector.tensor_tensor(out=y_all[:, i, cols], in0=y_ps[i, h][:], in1=b_all[:, cols], op=ALU.add)
 
-        def scalar_relu(i):
-            y = y_t[i][:, :SPLITS[i]]
+        def scalar_relu(i, cols):
+            y = y_all[:, i, cols]
             nc.scalar.activation(out=y, in_=y, func=ACT.Relu)
 
-        def scalar_squares(i):
-            totals[i] = stats.tile([P, 2], F32, name="totals")
-            s_products = unread.tile([P, SIZE], F32, name="s_products")
-            nc.scalar.activation(out=s_products[:, :SPLITS[i]], in_=y_t[i][:, :SPLITS[i]], func=ACT.Square,
-                                 accum_out=totals[i][:, 0:1])
+        def scalar_squares(i, cols, total):
+            s_products = unread.tile([P, SIZE + EXTRA], F32, name="s_products")
+            nc.scalar.activation(out=s_products[:, cols], in_=y_all[:, i, cols], func=ACT.Square, accum_out=total)
 
-        def vector_squares(i):
-            y = y_t[i][:, SPLITS[i]:]
-            v_products = unread.tile([P, SIZE], F32, name="v_products")
-            nc.vector.scalar_tensor_tensor(out=v_products[:, SPLITS[i]:], in0=y, scalar=0.0, in1=y,
-                                           op0=ALU.max, op1=ALU.mult, accum_out=totals[i][:, 1:2])
+        def vector_squares(i, cols, total):
+            y = y_all[:, i, cols]
+            v_products = unread.tile([P, SIZE + EXTRA], F32, name="v_products")
+            nc.vector.scalar_tensor_tensor(out=v_products[:, cols], in0=y, scalar=0.0, in1=y,
+                                           op0=ALU.max, op1=ALU.mult, accum_out=total)
 
-        def norm2_floor(i):
+        def new_m_sq(i):
             m_sq[i] = stats.tile([P, 1], F32, name="m_sq")
-            nc.vector.tensor_scalar(out=m_sq[i][:], in0=totals[i][:, 0:1], scalar1=totals[i][:, 1:2],
-                                    scalar2=EPS * EPS, op0=ALU.add, op1=ALU.max)
+            return m_sq[i][:]
 
         def norm2_root(i):
             inv_m[i] = stats.tile([P, 1], F32, name="inv_m")
@@ -227,15 +223,15 @@ def tile_graphconvhyp_pb_kernel(tc, mid, W, b, out):
             nc.scalar.activation(out=gain[i][:], in_=tanh_m[i][:], func=ACT.Copy, scale=inv_m[i][:, 0:1])
 
         def scale_on_vector(i, cols):
-            nc.vector.tensor_scalar(out=y_t[i][:, cols], in0=y_t[i][:, cols], scalar1=0.0,
+            nc.vector.tensor_scalar(out=y_all[:, i, cols], in0=y_all[:, i, cols], scalar1=0.0,
                                     scalar2=gain[i][:, 0:1], op0=ALU.max, op1=ALU.mult)
 
         def scale_on_scalar(i, cols):
-            nc.scalar.activation(out=y_t[i][:, cols], in_=y_t[i][:, cols], func=ACT.Relu,
+            nc.scalar.activation(out=y_all[:, i, cols], in_=y_all[:, i, cols], func=ACT.Relu,
                                  scale=gain[i][:, 0:1])
 
         def store(i, cols):
-            nc.sync.dma_start(out=out[i * P:(i + 1) * P, cols], in_=y_t[i][:, cols])
+            nc.sync.dma_start(out=out[i * P:(i + 1) * P, cols], in_=y_all[:, i, cols])
 
         def scale_out(i):
             whole = slice(0, SIZE)
@@ -249,79 +245,113 @@ def tile_graphconvhyp_pb_kernel(tc, mid, W, b, out):
         nc.vector.memset(b_row[:], 0.0)
         nc.vector.memset(one[:], 1.0)
         nc.vector.memset(ones[:], 1.0)
+        nc.gpsimd.memset(y_all[:, :, SIZE:SIZE + EXTRA], 1e-15)
         nc.gpsimd.memset(half[:], 0.5)
         nc.gpsimd.memset(minus_half[:], -0.5)
         make_identity(nc, ident[:])
         nc.scalar.activation(out=warm[:, 0:1], in_=one[:], func=ACT.Ln)
         load_rows(0)
         nc.sync.dma_start(out=b_row[0:1, :], in_=b.rearrange("(o n) -> o n", o=1))
-        for i in range(1, ROW_TILES):
-            load_rows(i)
-        for q in range(len(PIECES)):
-            load_w(q)
+        for load, which in ((load_rows, 1), (load_w, 0), (load_rows, 2), (load_w, 1), (load_rows, 3),
+                            (load_rows, 4), (load_w, 2), (load_w, 3), (load_rows, 5), (load_rows, 6), (load_rows, 7)):
+            load(which)
 
-        for i in range(ROW_TILES):
-            square_sum(i)
-        spread_ps()
+        square_sum(0)
+        square_sum(1)
         norm_root(0)
+        spread_ps()
+        square_sum(2)
         regroup_w(0)
         spread_copy()
+        square_sum(3)
         regroup_w(1)
-        quantise_w(0)
         norm_clip(0)
         norm_recip(0)
         log_terms(0)
-        nc.scalar.activation(out=warm[:, 1:2], in_=one[:], func=ACT.Tanh)
-        regroup_w(2)
+        quantise_w(0)
         log_ratios(0)
+        square_sum(4)
         for i in (0, 1):
             scale_rows(i)
             transpose_rows(i)
-            regroup_rows(i)
         quantise_w(1)
+        square_sum(5)
+        norm_root(1)
+        regroup_w(2)
+        regroup_rows(0)
+        regroup_rows(1)
         regroup_w(3)
-        for i in (2, 3):
-            scale_rows(i)
-            transpose_rows(i)
-            regroup_rows(i)
         quantise_w(2)
+        norm_clip(1)
+        norm_recip(1)
+        log_terms(1)
         quantise_rows(0)
         multiply(0, 0)
         quantise_rows(1)
+        log_ratios(1)
+        square_sum(6)
         quantise_w(3)
         multiply(0, 1)
-        multiply(1, 0)
-        multiply(1, 1)
-        for i in range(4, 4):
+        for i in (2, 3):
             scale_rows(i)
             transpose_rows(i)
-            regroup_rows(i)
-        quantise_rows(2)
+        multiply(1, 0)
+        multiply(1, 1)
+        square_sum(7)
+        norm_root(2)
+        regroup_rows(2)
+        regroup_rows(3)
+        for i in (4, 5):
+            scale_rows(i)
+            transpose_rows(i)
 
-        for r in range(ROW_TILES):
+        whole = slice(0, SIZE)
+        summed = slice(0, SIZE + EXTRA)
+        for r in range(LAST):
             add_bias(r, 0)
             add_bias(r, 1)
-            if 4 <= r + 4 < ROW_TILES:
-                scale_rows(r + 4)
-                transpose_rows(r + 4)
-            scalar_relu(r)
-            if r > 0:
-                out_tanh(r - 1)
-            scalar_squares(r)
-            if r > 0:
-                out_gain(r - 1)
-            if 4 <= r + 4 < ROW_TILES:
-                regroup_rows(r + 4)
+            if r == 0:
+                norm_clip(2)
+                norm_recip(2)
+                log_terms(2)
+                scalar_relu(0, whole)
             if r + 2 < ROW_TILES:
+                quantise_rows(r + 2)
                 multiply(r + 2, 0)
                 multiply(r + 2, 1)
-            vector_squares(r)
-            if r > 0:
+            if r == 0:
+                log_ratios(2)
+                scale_rows(6)
+                transpose_rows(6)
+                scale_rows(7)
+                transpose_rows(7)
+                scalar_squares(0, summed, new_m_sq(0))
+                nc.scalar.activation(out=warm[:, 1:2], in_=one[:], func=ACT.Tanh)
+                regroup_rows(4)
+            else:
+                out_tanh(r - 1)
+                if r in SCALAR_SUMS:
+                    scalar_relu(r, whole)
+                elif r + 4 < ROW_TILES:
+                    regroup_rows(r + 4)
+                out_gain(r - 1)
+                if r in SCALAR_SUMS:
+                    scalar_squares(r, summed, new_m_sq(r))
+                else:
+                    vector_squares(r, summed, new_m_sq(r))
                 scale_out(r - 1)
-            if r + 3 < ROW_TILES:
-                quantise_rows(r + 3)
-            norm2_floor(r)
             norm2_root(r)
+        sums = stats.tile([P, 2], F32, name="sums", bufs=1)
+        add_bias(LAST, 0)
+        out_tanh(LAST - 1)
+        scalar_relu(LAST, slice(0, BANK))
+        add_bias(LAST, 1)
+        out_gain(LAST - 1)
+        scalar_squares(LAST, slice(0, BANK), sums[:, 0:1])
+        vector_squares(LAST, slice(BANK, SIZE + EXTRA), sums[:, 1:2])
+        nc.vector.tensor_tensor(out=new_m_sq(LAST), in0=sums[:, 0:1], in1=sums[:, 1:2], op=ALU.add)
+        scale_out(LAST - 1)
+        norm2_root(LAST)
         out_tanh(LAST)
         out_gain(LAST)
         scale_on_scalar(LAST, slice(0, TAIL))

@@ -29,6 +29,7 @@ LAST = ROW_TILES - 1
 SCALAR_W = (3,)
 SCALAR_SUMS = (0, 4)
 TAIL = 384
+SPLIT = 384
 EXTRA = 1
 VECTOR_NORMS = (0,)
 VECTOR_REGROUPS = (0, 1)
@@ -39,8 +40,6 @@ def tile_graphconvhyp_pb_kernel(tc, mid, W, b, out):
     nc = tc.nc
     with ExitStack() as ctx:
         const = ctx.enter_context(tc.tile_pool(name="const", bufs=1))
-        rows_in = ctx.enter_context(tc.tile_pool(name="rows_in", bufs=ROW_TILES))
-        w_in = ctx.enter_context(tc.tile_pool(name="w_in", bufs=len(PIECES)))
         w_grouped = ctx.enter_context(tc.tile_pool(name="w_grouped", bufs=len(PIECES)))
         u_rows = ctx.enter_context(tc.tile_pool(name="u_rows", bufs=ROW_TILES))
         u_grouped = ctx.enter_context(tc.tile_pool(name="u_grouped", bufs=ROW_TILES))
@@ -49,6 +48,9 @@ def tile_graphconvhyp_pb_kernel(tc, mid, W, b, out):
         ps_t = ctx.enter_context(tc.psum_pool(name="ps_t", bufs=3))
         ps_y = ctx.enter_context(tc.psum_pool(name="ps_y", bufs=5))
 
+        mid_rows = mid.rearrange("(p i) k -> p i k", i=ROW_TILES)
+        out_rows = out.rearrange("(p i) n -> p i n", i=ROW_TILES)
+        mid_all = const.tile([P, ROW_TILES, SIZE], BF16, name="mid_all")
         ident = const.tile([P, P], F32, name="ident")
         ones = const.tile([P, P], BF16, name="ones")
         b_row = const.tile([P, SIZE], BF16, name="b_row")
@@ -63,25 +65,24 @@ def tile_graphconvhyp_pb_kernel(tc, mid, W, b, out):
         u_codes = const.tile([P, ROW_TILES, PASSES * P], U32, name="u_codes", align_bytes=64)
         u_scales = const.tile([P, ROW_TILES, PASSES * P], U8, name="u_scales", align_bytes=64)
 
-        mid_t, w_raw, w_grp, b_ps = {}, {}, {}, {}
+        w_raw, w_grp, b_ps = {}, {}, {}
         n_sq, n_raw, norm, half_inv, logs, ratio = {}, {}, {}, {}, {}, {}
         u_t, u_ps, u_grp, y_ps = {}, {}, {}, {}
         m_sq, inv_m, tanh_m, gain = {}, {}, {}, {}
         place = {i: (bt, c) for bt, batch in enumerate(BATCHES) for c, i in enumerate(batch)}
 
-        def load_rows(i):
-            mid_t[i] = rows_in.tile([P, SIZE], BF16, name="mid_t")
-            nc.sync.dma_start(out=mid_t[i][:], in_=mid[i * P:(i + 1) * P, :])
+        def load_rows(i, count):
+            nc.sync.dma_start(out=mid_all[:, i:i + count, :], in_=mid_rows[:, i:i + count, :])
 
-        def load_w(q):
-            g, h = PIECES[q]
-            w_raw[q] = w_in.tile([P, PACK, BANK], BF16, name="w_raw")
+        def load_w(g, halves):
+            cols = slice(halves[0] * BANK, (halves[-1] + 1) * BANK)
+            raw = const.tile([P, PACK, len(halves) * BANK], BF16, name="w_raw%d%d" % (g, halves[0]))
             nc.sync.dma_start(
-                out=w_raw[q][:],
-                in_=W[g * K_PASS:(g + 1) * K_PASS, h * BANK:(h + 1) * BANK].rearrange(
-                    "(p t) n -> p t n", t=PACK, p=P
-                ),
+                out=raw[:],
+                in_=W[g * K_PASS:(g + 1) * K_PASS, cols].rearrange("(p t) n -> p t n", t=PACK, p=P),
             )
+            for c, h in enumerate(halves):
+                w_raw[g, h] = raw[:, :, c * BANK:(c + 1) * BANK]
 
         def spread_ps():
             b_ps["b"] = ps_y.tile([P, SIZE], BF16, name="b_ps", tag="y_ps")
@@ -91,14 +92,15 @@ def tile_graphconvhyp_pb_kernel(tc, mid, W, b, out):
                                  start=True, stop=True)
 
         def spread_copy():
-            nc.vector.tensor_copy(out=b_all[:], in_=b_ps["b"][:])
+            nc.scalar.copy(out=b_all[:], in_=b_ps["b"][:])
 
         def regroup_w(q):
+            g, h = PIECES[q]
             w_grp[q] = w_grouped.tile([P, BANK, PACK], BF16, name="w_grp", align_bytes=64)
             copy = nc.scalar.copy if q in SCALAR_W else nc.vector.tensor_copy
             copy(
                 out=w_grp[q][:].rearrange("p (c i) t -> p c t i", i=4),
-                in_=w_raw[q][:].rearrange("p t (c i) -> p c t i", i=4),
+                in_=w_raw[g, h].rearrange("p t (c i) -> p c t i", i=4),
             )
 
         def quantise_w(q):
@@ -116,11 +118,11 @@ def tile_graphconvhyp_pb_kernel(tc, mid, W, b, out):
             total = n_sq[bt][:, c:c + 1]
             if i in VECTOR_NORMS:
                 v_squares = unread.tile([P, SIZE], BF16, name="v_squares")
-                nc.vector.scalar_tensor_tensor(out=v_squares[:], in0=mid_t[i][:], scalar=4.0, in1=mid_t[i][:],
+                nc.vector.scalar_tensor_tensor(out=v_squares[:], in0=mid_all[:, i, :], scalar=4.0, in1=mid_all[:, i, :],
                                                op0=ALU.mult, op1=ALU.mult, accum_out=total)
             else:
                 s_squares = unread.tile([P, SIZE], BF16, name="s_squares")
-                nc.scalar.activation(out=s_squares[:], in_=mid_t[i][:], func=ACT.Square, scale=2.0, accum_out=total)
+                nc.scalar.activation(out=s_squares[:], in_=mid_all[:, i, :], func=ACT.Square, scale=2.0, accum_out=total)
 
         def norm_root(bt):
             w = len(BATCHES[bt])
@@ -149,7 +151,7 @@ def tile_graphconvhyp_pb_kernel(tc, mid, W, b, out):
         def scale_rows(i):
             bt, c = place[i]
             u_t[i] = u_rows.tile([P, SIZE], BF16, name="u_t")
-            nc.vector.tensor_scalar(out=u_t[i][:], in0=mid_t[i][:], scalar1=ratio[bt][:, c:c + 1],
+            nc.vector.tensor_scalar(out=u_t[i][:], in0=mid_all[:, i, :], scalar1=ratio[bt][:, c:c + 1],
                                     scalar2=half_inv[bt][:, c:c + 1], op0=ALU.mult, op1=ALU.mult)
 
         def transpose_rows(i):
@@ -231,7 +233,7 @@ def tile_graphconvhyp_pb_kernel(tc, mid, W, b, out):
                                  scale=gain[i][:, 0:1])
 
         def store(i, cols):
-            nc.sync.dma_start(out=out[i * P:(i + 1) * P, cols], in_=y_all[:, i, cols])
+            nc.sync.dma_start(out=out_rows[:, i, cols], in_=y_all[:, i, cols])
 
         def scale_out(i):
             whole = slice(0, SIZE)
@@ -242,7 +244,7 @@ def tile_graphconvhyp_pb_kernel(tc, mid, W, b, out):
             store(i, whole)
 
         ctx.enter_context(tc.manual_schedule())
-        nc.vector.memset(b_row[:], 0.0)
+        nc.vector.memset(b_row[:].bitcast(U32), 0)
         nc.vector.memset(one[:], 1.0)
         nc.vector.memset(ones[:], 1.0)
         nc.gpsimd.memset(y_all[:, :, SIZE:SIZE + EXTRA], 1e-15)
@@ -250,25 +252,30 @@ def tile_graphconvhyp_pb_kernel(tc, mid, W, b, out):
         nc.gpsimd.memset(minus_half[:], -0.5)
         make_identity(nc, ident[:])
         nc.scalar.activation(out=warm[:, 0:1], in_=one[:], func=ACT.Ln)
-        load_rows(0)
+        load_rows(0, 1)
         nc.sync.dma_start(out=b_row[0:1, :], in_=b.rearrange("(o n) -> o n", o=1))
-        for load, which in ((load_rows, 1), (load_w, 0), (load_rows, 2), (load_w, 1), (load_rows, 3),
-                            (load_rows, 4), (load_w, 2), (load_w, 3), (load_rows, 5), (load_rows, 6), (load_rows, 7)):
-            load(which)
+        load_rows(1, 1)
+        load_w(0, (0,))
+        load_rows(2, 2)
+        load_w(1, (0,))
+        load_rows(4, 2)
+        load_w(0, (1,))
+        load_w(1, (1,))
+        load_rows(6, 2)
 
         square_sum(0)
         square_sum(1)
         norm_root(0)
         spread_ps()
+        spread_copy()
         square_sum(2)
         regroup_w(0)
-        spread_copy()
+        quantise_w(0)
         square_sum(3)
         regroup_w(1)
         norm_clip(0)
         norm_recip(0)
         log_terms(0)
-        quantise_w(0)
         log_ratios(0)
         square_sum(4)
         for i in (0, 1):
@@ -343,14 +350,14 @@ def tile_graphconvhyp_pb_kernel(tc, mid, W, b, out):
             norm2_root(r)
         sums = stats.tile([P, 2], F32, name="sums", bufs=1)
         add_bias(LAST, 0)
+        scalar_relu(LAST, slice(0, SPLIT))
         out_tanh(LAST - 1)
-        scalar_relu(LAST, slice(0, BANK))
         add_bias(LAST, 1)
         out_gain(LAST - 1)
-        scalar_squares(LAST, slice(0, BANK), sums[:, 0:1])
-        vector_squares(LAST, slice(BANK, SIZE + EXTRA), sums[:, 1:2])
-        nc.vector.tensor_tensor(out=new_m_sq(LAST), in0=sums[:, 0:1], in1=sums[:, 1:2], op=ALU.add)
+        scalar_squares(LAST, slice(0, SPLIT), sums[:, 0:1])
+        vector_squares(LAST, slice(SPLIT, SIZE + EXTRA), sums[:, 1:2])
         scale_out(LAST - 1)
+        nc.vector.tensor_tensor(out=new_m_sq(LAST), in0=sums[:, 0:1], in1=sums[:, 1:2], op=ALU.add)
         norm2_root(LAST)
         out_tanh(LAST)
         out_gain(LAST)

@@ -29,7 +29,6 @@ LAST = ROW_TILES - 1
 SCALAR_W = (3,)
 SCALAR_SUMS = (0, 4)
 TAIL = 384
-SPLIT = 384
 EXTRA = 1
 VECTOR_NORMS = (0,)
 VECTOR_REGROUPS = (0, 1)
@@ -92,7 +91,13 @@ def tile_graphconvhyp_pb_kernel(tc, mid, W, b, out):
                                  start=True, stop=True)
 
         def spread_copy():
-            nc.scalar.copy(out=b_all[:], in_=b_ps["b"][:])
+            nc.vector.tensor_copy(out=b_all[:], in_=b_ps["b"][:])
+
+        def warm_tensor(q, count):
+            scratch = ps_y.tile([P, BANK], F32, name="scratch", tag="y_ps")
+            for c in range(count):
+                nc.tensor.matmul(out=scratch[:], lhsT=ones[:], rhs=w_grp[q][:, c * P:(c + 1) * P, :].rearrange("p n t -> p (n t)"),
+                                 start=True, stop=True)
 
         def regroup_w(q):
             g, h = PIECES[q]
@@ -267,24 +272,25 @@ def tile_graphconvhyp_pb_kernel(tc, mid, W, b, out):
         square_sum(1)
         norm_root(0)
         spread_ps()
-        spread_copy()
         square_sum(2)
         regroup_w(0)
+        spread_copy()
         quantise_w(0)
         square_sum(3)
         regroup_w(1)
         norm_clip(0)
         norm_recip(0)
         log_terms(0)
+        quantise_w(1)
         log_ratios(0)
         square_sum(4)
         for i in (0, 1):
             scale_rows(i)
             transpose_rows(i)
-        quantise_w(1)
         square_sum(5)
         norm_root(1)
         regroup_w(2)
+        warm_tensor(2, 2)
         regroup_rows(0)
         regroup_rows(1)
         regroup_w(3)
@@ -348,20 +354,16 @@ def tile_graphconvhyp_pb_kernel(tc, mid, W, b, out):
                     vector_squares(r, summed, new_m_sq(r))
                 scale_out(r - 1)
             norm2_root(r)
-        sums = stats.tile([P, 2], F32, name="sums", bufs=1)
         add_bias(LAST, 0)
-        scalar_relu(LAST, slice(0, SPLIT))
-        out_tanh(LAST - 1)
         add_bias(LAST, 1)
+        out_tanh(LAST - 1)
         out_gain(LAST - 1)
-        scalar_squares(LAST, slice(0, SPLIT), sums[:, 0:1])
-        vector_squares(LAST, slice(SPLIT, SIZE + EXTRA), sums[:, 1:2])
+        vector_squares(LAST, summed, new_m_sq(LAST))
         scale_out(LAST - 1)
-        nc.vector.tensor_tensor(out=new_m_sq(LAST), in0=sums[:, 0:1], in1=sums[:, 1:2], op=ALU.add)
         norm2_root(LAST)
         out_tanh(LAST)
         out_gain(LAST)
-        scale_on_scalar(LAST, slice(0, TAIL))
-        store(LAST, slice(0, TAIL))
         scale_on_vector(LAST, slice(TAIL, SIZE))
         store(LAST, slice(TAIL, SIZE))
+        scale_on_scalar(LAST, slice(0, TAIL))
+        store(LAST, slice(0, TAIL))

@@ -296,10 +296,10 @@ def tile_graphconvhyp_pb_kernel(tc, mid, W, b, out):
         regroup_w(3)
         quantise_w(2)
         norm_clip(1)
-        norm_recip(1)
-        log_terms(1)
         quantise_rows(0)
         multiply(0, 0)
+        norm_recip(1)
+        log_terms(1)
         quantise_rows(1)
         log_ratios(1)
         square_sum(6)
@@ -324,36 +324,56 @@ def tile_graphconvhyp_pb_kernel(tc, mid, W, b, out):
             add_bias(r, 0)
             add_bias(r, 1)
             if r == 0:
+                scalar_relu(0, whole)
+
+                continue
+            if r == 1:
                 norm_clip(2)
+                quantise_rows(2)
+                multiply(2, 0)
+                multiply(2, 1)
                 norm_recip(2)
                 log_terms(2)
-                scalar_relu(0, whole)
+                regroup_rows(4)
+                scalar_squares(0, summed, new_m_sq(0))
+                nc.scalar.activation(out=warm[:, 1:2], in_=one[:], func=ACT.Tanh)
+                quantise_rows(3)
+                multiply(3, 0)
+                multiply(3, 1)
+                vector_squares(1, summed, new_m_sq(1))
+                log_ratios(2)
+                for i in (6, 7):
+                    scale_rows(i)
+                    transpose_rows(i)
+                norm2_root(0)
+                norm2_root(1)
+                regroup_rows(5)
+                continue
             if r + 2 < ROW_TILES:
                 quantise_rows(r + 2)
                 multiply(r + 2, 0)
                 multiply(r + 2, 1)
-            if r == 0:
-                log_ratios(2)
-                scale_rows(6)
-                transpose_rows(6)
-                scale_rows(7)
-                transpose_rows(7)
-                scalar_squares(0, summed, new_m_sq(0))
-                nc.scalar.activation(out=warm[:, 1:2], in_=one[:], func=ACT.Tanh)
-                regroup_rows(4)
+            done = [t for t in (r - 2, r - 1) if t + (2 if t in (0,) + SCALAR_SUMS[1:] else 1) == r]
+            for t in done:
+                out_tanh(t)
+            if r in SCALAR_SUMS:
+                scalar_relu(r, whole)
+            if r == 2:
+                regroup_rows(6)
+            if r == 3:
+                regroup_rows(7)
+            for t in done:
+                out_gain(t)
+            if r in SCALAR_SUMS:
+                scalar_squares(r, summed, new_m_sq(r))
             else:
-                out_tanh(r - 1)
-                if r in SCALAR_SUMS:
-                    scalar_relu(r, whole)
-                elif r + 4 < ROW_TILES:
-                    regroup_rows(r + 4)
-                out_gain(r - 1)
-                if r in SCALAR_SUMS:
-                    scalar_squares(r, summed, new_m_sq(r))
-                else:
-                    vector_squares(r, summed, new_m_sq(r))
-                scale_out(r - 1)
-            norm2_root(r)
+                vector_squares(r, summed, new_m_sq(r))
+            for t in done:
+                scale_out(t)
+            if r not in SCALAR_SUMS:
+                norm2_root(r)
+            if r - 1 in SCALAR_SUMS:
+                norm2_root(r - 1)
         add_bias(LAST, 0)
         add_bias(LAST, 1)
         out_tanh(LAST - 1)

@@ -104,8 +104,8 @@ def tile_graphconvhyp_pb_kernel(tc, mid, W, b, out):
             w_grp[q] = w_grouped.tile([P, BANK, PACK], BF16, name="w_grp", align_bytes=64)
             copy = nc.scalar.copy if q in SCALAR_W else nc.vector.tensor_copy
             copy(
-                out=w_grp[q][:].rearrange("p (c i) t -> p c t i", i=4),
-                in_=w_raw[g, h].rearrange("p t (c i) -> p c t i", i=4),
+                out=w_grp[q][:].rearrange("p (c i) t -> p c t i", i=8),
+                in_=w_raw[g, h].rearrange("p t (c i) -> p c t i", i=8),
             )
 
         def quantise_w(q):

@@ -257,9 +257,8 @@ def tile_graphconvhyp_pb_kernel(tc, mid, W, b, out):
         nc.gpsimd.memset(minus_half[:], -0.5)
         make_identity(nc, ident[:])
         nc.scalar.activation(out=warm[:, 0:1], in_=one[:], func=ACT.Ln)
-        load_rows(0, 1)
+        load_rows(0, 2)
         nc.sync.dma_start(out=b_row[0:1, :], in_=b.rearrange("(o n) -> o n", o=1))
-        load_rows(1, 1)
         load_w(0, (0,))
         load_rows(2, 2)
         load_w(1, (0,))
@@ -369,7 +368,10 @@ def tile_graphconvhyp_pb_kernel(tc, mid, W, b, out):
             else:
                 vector_squares(r, summed, new_m_sq(r))
             for t in done:
-                scale_out(t)
+                if t == LAST - 2:
+                    scale_on_scalar(t, slice(0, BANK))
+                else:
+                    scale_out(t)
             if r not in SCALAR_SUMS:
                 norm2_root(r)
             if r - 1 in SCALAR_SUMS:
@@ -377,6 +379,8 @@ def tile_graphconvhyp_pb_kernel(tc, mid, W, b, out):
         add_bias(LAST, 0)
         add_bias(LAST, 1)
         out_tanh(LAST - 1)
+        scale_on_scalar(LAST - 2, slice(BANK, SIZE))
+        store(LAST - 2, whole)
         out_gain(LAST - 1)
         vector_squares(LAST, summed, new_m_sq(LAST))
         scale_out(LAST - 1)

@@ -27,7 +27,7 @@ PIECES = [(0, 0), (1, 0), (0, 1), (1, 1)]
 BATCHES = [(0, 1), (2, 3, 4, 5), (6, 7)]
 LAST = ROW_TILES - 1
 SCALAR_W = (3,)
-SCALAR_SUMS = (0, 4)
+SCALAR_SUMS = (0, 2)
 TAIL = 384
 EXTRA = 1
 VECTOR_NORMS = (0,)
@@ -319,6 +319,7 @@ def tile_graphconvhyp_pb_kernel(tc, mid, W, b, out):
 
         whole = slice(0, SIZE)
         summed = slice(0, SIZE + EXTRA)
+        half_done = None
         for r in range(LAST):
             add_bias(r, 0)
             add_bias(r, 1)
@@ -355,23 +356,26 @@ def tile_graphconvhyp_pb_kernel(tc, mid, W, b, out):
             done = [t for t in (r - 2, r - 1) if t + (2 if t in (0,) + SCALAR_SUMS[1:] else 1) == r]
             for t in done:
                 out_tanh(t)
-            if r in SCALAR_SUMS:
-                scalar_relu(r, whole)
+            if half_done is not None:
+                scale_on_scalar(half_done, slice(BANK, SIZE))
+                store(half_done, whole)
             if r == 2:
                 regroup_rows(6)
-            if r == 3:
-                regroup_rows(7)
             for t in done:
                 out_gain(t)
+            if r == 3:
+                regroup_rows(7)
+            if r in SCALAR_SUMS:
+                scalar_relu(r, whole)
+            for t in done[:-1]:
+                scale_out(t)
+            half_done = done[-1] if done else None
+            if half_done is not None:
+                scale_on_scalar(half_done, slice(0, BANK))
             if r in SCALAR_SUMS:
                 scalar_squares(r, summed, new_m_sq(r))
             else:
                 vector_squares(r, summed, new_m_sq(r))
-            for t in done:
-                if t == LAST - 2:
-                    scale_on_scalar(t, slice(0, BANK))
-                else:
-                    scale_out(t)
             if r not in SCALAR_SUMS:
                 norm2_root(r)
             if r - 1 in SCALAR_SUMS:
@@ -379,8 +383,8 @@ def tile_graphconvhyp_pb_kernel(tc, mid, W, b, out):
         add_bias(LAST, 0)
         add_bias(LAST, 1)
         out_tanh(LAST - 1)
-        scale_on_scalar(LAST - 2, slice(BANK, SIZE))
-        store(LAST - 2, whole)
+        scale_on_scalar(half_done, slice(BANK, SIZE))
+        store(half_done, whole)
         out_gain(LAST - 1)
         vector_squares(LAST, summed, new_m_sq(LAST))
         scale_out(LAST - 1)

@@ -32,7 +32,6 @@ TAIL = 384
 EXTRA = 1
 VECTOR_NORMS = (0,)
 VECTOR_REGROUPS = (0, 1)
-VECTOR_OUTS = ()
 
 
 def tile_graphconvhyp_pb_kernel(tc, mid, W, b, out):
@@ -240,14 +239,6 @@ def tile_graphconvhyp_pb_kernel(tc, mid, W, b, out):
         def store(i, cols):
             nc.sync.dma_start(out=out_rows[:, i, cols], in_=y_all[:, i, cols])
 
-        def scale_out(i):
-            whole = slice(0, SIZE)
-            if i in VECTOR_OUTS:
-                scale_on_vector(i, whole)
-            else:
-                scale_on_scalar(i, whole)
-            store(i, whole)
-
         ctx.enter_context(tc.manual_schedule())
         nc.vector.memset(b_row[:].bitcast(U32), 0)
         nc.vector.memset(one[:], 1.0)
@@ -272,8 +263,8 @@ def tile_graphconvhyp_pb_kernel(tc, mid, W, b, out):
         norm_root(0)
         spread_ps()
         square_sum(2)
-        regroup_w(0)
         spread_copy()
+        regroup_w(0)
         quantise_w(0)
         square_sum(3)
         regroup_w(1)
@@ -319,79 +310,109 @@ def tile_graphconvhyp_pb_kernel(tc, mid, W, b, out):
 
         whole = slice(0, SIZE)
         summed = slice(0, SIZE + EXTRA)
-        half_done = None
-        for r in range(LAST):
-            add_bias(r, 0)
-            add_bias(r, 1)
-            if r == 0:
-                scalar_relu(0, whole)
-
-                continue
-            if r == 1:
-                norm_clip(2)
-                quantise_rows(2)
-                multiply(2, 0)
-                multiply(2, 1)
-                norm_recip(2)
-                log_terms(2)
-                regroup_rows(4)
-                scalar_squares(0, summed, new_m_sq(0))
-                nc.scalar.activation(out=warm[:, 1:2], in_=one[:], func=ACT.Tanh)
-                quantise_rows(3)
-                multiply(3, 0)
-                multiply(3, 1)
-                vector_squares(1, summed, new_m_sq(1))
-                log_ratios(2)
-                for i in (6, 7):
-                    scale_rows(i)
-                    transpose_rows(i)
-                norm2_root(0)
-                norm2_root(1)
-                regroup_rows(5)
-                continue
-            if r + 2 < ROW_TILES:
-                quantise_rows(r + 2)
-                multiply(r + 2, 0)
-                multiply(r + 2, 1)
-            done = [t for t in (r - 2, r - 1) if t + (2 if t in (0,) + SCALAR_SUMS[1:] else 1) == r]
-            for t in done:
-                out_tanh(t)
-            if half_done is not None:
-                scale_on_scalar(half_done, slice(BANK, SIZE))
-                store(half_done, whole)
-            if r == 2:
-                regroup_rows(6)
-            for t in done:
-                out_gain(t)
-            if r == 3:
-                regroup_rows(7)
-            if r in SCALAR_SUMS:
-                scalar_relu(r, whole)
-            for t in done[:-1]:
-                scale_out(t)
-            half_done = done[-1] if done else None
-            if half_done is not None:
-                scale_on_scalar(half_done, slice(0, BANK))
-            if r in SCALAR_SUMS:
-                scalar_squares(r, summed, new_m_sq(r))
-            else:
-                vector_squares(r, summed, new_m_sq(r))
-            if r not in SCALAR_SUMS:
-                norm2_root(r)
-            if r - 1 in SCALAR_SUMS:
-                norm2_root(r - 1)
-        add_bias(LAST, 0)
-        add_bias(LAST, 1)
-        out_tanh(LAST - 1)
-        scale_on_scalar(half_done, slice(BANK, SIZE))
-        store(half_done, whole)
-        out_gain(LAST - 1)
-        vector_squares(LAST, summed, new_m_sq(LAST))
-        scale_out(LAST - 1)
-        norm2_root(LAST)
-        out_tanh(LAST)
-        out_gain(LAST)
-        scale_on_vector(LAST, slice(TAIL, SIZE))
-        store(LAST, slice(TAIL, SIZE))
-        scale_on_scalar(LAST, slice(0, TAIL))
-        store(LAST, slice(0, TAIL))
+        left, right = slice(0, BANK), slice(BANK, SIZE)
+        add_bias(0, 0)
+        add_bias(0, 1)
+        scalar_relu(0, whole)
+        add_bias(1, 0)
+        add_bias(1, 1)
+        norm_clip(2)
+        quantise_rows(2)
+        multiply(2, 0)
+        multiply(2, 1)
+        norm_recip(2)
+        log_terms(2)
+        regroup_rows(4)
+        scalar_squares(0, summed, new_m_sq(0))
+        nc.scalar.activation(out=warm[:, 1:2], in_=one[:], func=ACT.Tanh)
+        quantise_rows(3)
+        multiply(3, 0)
+        multiply(3, 1)
+        log_ratios(2)
+        vector_squares(1, summed, new_m_sq(1))
+        for i in (6, 7):
+            scale_rows(i)
+            transpose_rows(i)
+        add_bias(2, 0)
+        norm2_root(0)
+        norm2_root(1)
+        regroup_rows(5)
+        add_bias(2, 1)
+        add_bias(3, 0)
+        quantise_rows(4)
+        multiply(4, 0)
+        multiply(4, 1)
+        out_tanh(0)
+        out_tanh(1)
+        regroup_rows(6)
+        out_gain(0)
+        out_gain(1)
+        scalar_relu(2, whole)
+        scale_on_scalar(0, left)
+        scalar_squares(2, summed, new_m_sq(2))
+        scale_on_scalar(0, right)
+        store(0, whole)
+        regroup_rows(7)
+        scale_on_scalar(1, left)
+        add_bias(3, 1)
+        quantise_rows(5)
+        multiply(5, 0)
+        multiply(5, 1)
+        scale_on_scalar(1, right)
+        store(1, whole)
+        vector_squares(3, summed, new_m_sq(3))
+        norm2_root(3)
+        norm2_root(2)
+        add_bias(4, 0)
+        add_bias(4, 1)
+        quantise_rows(6)
+        multiply(6, 0)
+        multiply(6, 1)
+        vector_squares(4, summed, new_m_sq(4))
+        norm2_root(4)
+        add_bias(5, 0)
+        add_bias(5, 1)
+        quantise_rows(7)
+        multiply(7, 0)
+        multiply(7, 1)
+        out_tanh(3)
+        out_tanh(2)
+        out_gain(3)
+        out_gain(2)
+        scale_on_scalar(2, whole)
+        store(2, whole)
+        scale_on_scalar(3, left)
+        out_tanh(4)
+        vector_squares(5, summed, new_m_sq(5))
+        norm2_root(5)
+        add_bias(6, 0)
+        scale_on_scalar(3, right)
+        store(3, whole)
+        out_gain(4)
+        add_bias(6, 1)
+        add_bias(7, 0)
+        scale_on_scalar(4, left)
+        out_tanh(5)
+        scale_on_scalar(4, right)
+        store(4, whole)
+        out_gain(5)
+        vector_squares(6, summed, new_m_sq(6))
+        norm2_root(6)
+        add_bias(7, 1)
+        scale_on_scalar(5, left)
+        scale_on_vector(5, right)
+        store(5, whole)
+        out_tanh(6)
+        out_gain(6)
+        vector_squares(7, summed, new_m_sq(7))
+        norm2_root(7)
+        scale_on_scalar(6, left)
+        store(6, left)
+        out_tanh(7)
+        scale_on_vector(6, right)
+        store(6, right)
+        out_gain(7)
+        scale_on_vector(7, slice(TAIL, SIZE))
+        store(7, slice(TAIL, SIZE))
+        scale_on_scalar(7, slice(0, TAIL))
+        store(7, slice(0, TAIL))

@@ -262,18 +262,18 @@ def tile_graphconvhyp_pb_kernel(tc, mid, W, b, out):
         square_sum(1)
         norm_root(0)
         spread_ps()
-        square_sum(2)
         spread_copy()
+        square_sum(2)
         regroup_w(0)
+        norm_clip(0)
+        log_terms(0)
         quantise_w(0)
         square_sum(3)
-        regroup_w(1)
-        norm_clip(0)
         norm_recip(0)
-        log_terms(0)
-        quantise_w(1)
+        regroup_w(1)
         log_ratios(0)
         square_sum(4)
+        quantise_w(1)
         for i in (0, 1):
             scale_rows(i)
             transpose_rows(i)
@@ -407,10 +407,9 @@ def tile_graphconvhyp_pb_kernel(tc, mid, W, b, out):
         vector_squares(7, summed, new_m_sq(7))
         norm2_root(7)
         scale_on_scalar(6, left)
-        store(6, left)
-        out_tanh(7)
         scale_on_vector(6, right)
-        store(6, right)
+        store(6, whole)
+        out_tanh(7)
         out_gain(7)
         scale_on_vector(7, slice(TAIL, SIZE))
         store(7, slice(TAIL, SIZE))

from contextlib import ExitStack

import concourse.mybir as mybir
from concourse.masks import make_identity

FLOPS = 2 * 1024 * 1024 * 1024

F32 = mybir.dt.float32
BF16 = mybir.dt.bfloat16
U32 = mybir.dt.uint32
U8 = mybir.dt.uint8
FP8X4 = mybir.dt.float8_e4m3fn_x4
ALU = mybir.AluOpType
ACT = mybir.ActivationFunctionType

P = 128
SIZE = 1024
ROW_TILES = SIZE // P
PACK = 4
PAIRS = 2
K_PASS = P * PACK
PASSES = SIZE // K_PASS
BANK = 512
HALVES = SIZE // BANK
EPS = 1e-7
PIECES = [(0, 0), (1, 0), (0, 1), (1, 1)]
BATCHES = [(0, 1), (2, 3, 4, 5), (6, 7)]
LAST = ROW_TILES - 1
SCALAR_W = (3,)
SCALAR_SUMS = (0, 2)
TAIL = 384
EXTRA = 1
VECTOR_NORMS = (0,)
VECTOR_REGROUPS = (0, 1)


def tile_graphconvhyp_pb_kernel(tc, mid, W, b, out):
    nc = tc.nc
    with ExitStack() as ctx:
        const = ctx.enter_context(tc.tile_pool(name="const", bufs=1))
        w_grouped = ctx.enter_context(tc.tile_pool(name="w_grouped", bufs=len(PIECES)))
        u_rows = ctx.enter_context(tc.tile_pool(name="u_rows", bufs=ROW_TILES))
        u_grouped = ctx.enter_context(tc.tile_pool(name="u_grouped", bufs=ROW_TILES))
        unread = ctx.enter_context(tc.tile_pool(name="unread", bufs=2))
        stats = ctx.enter_context(tc.tile_pool(name="stats", bufs=ROW_TILES))
        ps_t = ctx.enter_context(tc.psum_pool(name="ps_t", bufs=3))
        ps_y = ctx.enter_context(tc.psum_pool(name="ps_y", bufs=5))

        mid_rows = mid.rearrange("(p i) k -> p i k", i=ROW_TILES)
        out_rows = out.rearrange("(p i) n -> p i n", i=ROW_TILES)
        mid_all = const.tile([P, ROW_TILES, SIZE], BF16, name="mid_all")
        ident = const.tile([P, P], F32, name="ident")
        ones = const.tile([P, P], BF16, name="ones")
        b_row = const.tile([P, SIZE], BF16, name="b_row")
        b_all = const.tile([P, SIZE], BF16, name="b_all")
        one = const.tile([P, 1], F32, name="one")
        warm = const.tile([P, 2], F32, name="warm")
        half = const.tile([P, ROW_TILES], F32, name="half")
        minus_half = const.tile([P, ROW_TILES], F32, name="minus_half")
        w_codes = const.tile([P, PASSES, SIZE], U32, name="w_codes", align_bytes=64)
        w_scales = const.tile([P, PASSES, SIZE], U8, name="w_scales", align_bytes=64)
        y_all = const.tile([P, ROW_TILES, SIZE + EXTRA], F32, name="y_all")
        u_codes = const.tile([P, ROW_TILES, PASSES * P], U32, name="u_codes", align_bytes=64)
        u_scales = const.tile([P, ROW_TILES, PASSES * P], U8, name="u_scales", align_bytes=64)

        w_raw, w_grp, b_ps = {}, {}, {}
        n_sq, n_raw, norm, half_inv, logs, ratio = {}, {}, {}, {}, {}, {}
        u_t, u_ps, u_grp, y_ps = {}, {}, {}, {}
        m_sq, inv_m, tanh_m, gain = {}, {}, {}, {}
        place = {i: (bt, c) for bt, batch in enumerate(BATCHES) for c, i in enumerate(batch)}

        def load_rows(i, count):
            nc.sync.dma_start(out=mid_all[:, i:i + count, :], in_=mid_rows[:, i:i + count, :])

        def load_w(g, halves):
            cols = slice(halves[0] * BANK, (halves[-1] + 1) * BANK)
            raw = const.tile([P, PACK, len(halves) * BANK], BF16, name="w_raw%d%d" % (g, halves[0]))
            nc.sync.dma_start(
                out=raw[:],
                in_=W[g * K_PASS:(g + 1) * K_PASS, cols].rearrange("(p t) n -> p t n", t=PACK, p=P),
            )
            for c, h in enumerate(halves):
                w_raw[g, h] = raw[:, :, c * BANK:(c + 1) * BANK]

        def spread_ps():
            b_ps["b"] = ps_y.tile([P, SIZE], BF16, name="b_ps", tag="y_ps")
            for h in range(HALVES):
                cols = slice(h * BANK, (h + 1) * BANK)
                nc.tensor.matmul(out=b_ps["b"][:, cols], lhsT=ones[:], rhs=b_row[:, cols],
                                 start=True, stop=True)

        def spread_copy():
            nc.vector.tensor_copy(out=b_all[:], in_=b_ps["b"][:])

        def warm_tensor(q, count):
            scratch = ps_y.tile([P, BANK], F32, name="scratch", tag="y_ps")
            for c in range(count):
                nc.tensor.matmul(out=scratch[:], lhsT=ones[:], rhs=w_grp[q][:, c * P:(c + 1) * P, :].rearrange("p n t -> p (n t)"),
                                 start=True, stop=True)

        def regroup_w(q):
            g, h = PIECES[q]
            w_grp[q] = w_grouped.tile([P, BANK, PACK], BF16, name="w_grp", align_bytes=64)
            copy = nc.scalar.copy if q in SCALAR_W else nc.vector.tensor_copy
            copy(
                out=w_grp[q][:].rearrange("p (c i) t -> p c t i", i=8),
                in_=w_raw[g, h].rearrange("p t (c i) -> p c t i", i=8),
            )

        def quantise_w(q):
            g, h = PIECES[q]
            nc.vector.quantize_mx(
                out=w_codes[:, g, h * BANK:(h + 1) * BANK].bitcast(FP8X4),
                scales=w_scales[:, g, h * BANK:(h + 1) * BANK],
                in_=w_grp[q][:].rearrange("p n t -> p (n t)"),
            )

        def square_sum(i):
            bt, c = place[i]
            if c == 0:
                n_sq[bt] = stats.tile([P, len(BATCHES[bt])], F32, name="n_sq", tag="n_sq%d" % bt, bufs=1)
            total = n_sq[bt][:, c:c + 1]
            if i in VECTOR_NORMS:
                v_squares = unread.tile([P, SIZE], BF16, name="v_squares")
                nc.vector.scalar_tensor_tensor(out=v_squares[:], in0=mid_all[:, i, :], scalar=4.0, in1=mid_all[:, i, :],
                                               op0=ALU.mult, op1=ALU.mult, accum_out=total)
            else:
                s_squares = unread.tile([P, SIZE], BF16, name="s_squares")
                nc.scalar.activation(out=s_squares[:], in_=mid_all[:, i, :], func=ACT.Square, scale=2.0, accum_out=total)

        def norm_root(bt):
            w = len(BATCHES[bt])
            n_raw[bt] = stats.tile([P, w], F32, name="n_raw", tag="n_raw%d" % bt, bufs=1)
            nc.gpsimd.tensor_tensor(out=n_raw[bt][:], in0=n_sq[bt][:], in1=half[:, :w], op=ALU.pow)

        def norm_clip(bt):
            norm[bt] = stats.tile([P, len(BATCHES[bt])], F32, name="norm", tag="norm%d" % bt, bufs=1)
            nc.vector.tensor_scalar(out=norm[bt][:], in0=n_raw[bt][:], scalar1=2.0 * (1.0 - EPS),
                                    scalar2=2.0 * EPS, op0=ALU.min, op1=ALU.max)

        def norm_recip(bt):
            half_inv[bt] = stats.tile([P, len(BATCHES[bt])], F32, name="half_inv", tag="half_inv%d" % bt, bufs=1)
            nc.vector.reciprocal(out=half_inv[bt][:], in_=norm[bt][:])

        def log_terms(bt):
            w = len(BATCHES[bt])
            logs[bt] = stats.tile([P, 2, w], F32, name="logs", tag="logs%d" % bt, bufs=1)
            nc.scalar.activation(out=logs[bt][:, 0, :], in_=norm[bt][:], func=ACT.Ln, scale=0.5, bias=one[:, 0:1])
            nc.scalar.activation(out=logs[bt][:, 1, :], in_=norm[bt][:], func=ACT.Ln, scale=-0.5, bias=one[:, 0:1])

        def log_ratios(bt):
            ratio[bt] = stats.tile([P, len(BATCHES[bt])], F32, name="ratio", tag="ratio%d" % bt, bufs=1)
            nc.vector.tensor_tensor(out=ratio[bt][:], in0=logs[bt][:, 0, :], in1=logs[bt][:, 1, :], op=ALU.subtract)

        def scale_rows(i):
            bt, c = place[i]
            u_t[i] = u_rows.tile([P, SIZE], BF16, name="u_t")
            nc.vector.tensor_scalar(out=u_t[i][:], in0=mid_all[:, i, :], scalar1=ratio[bt][:, c:c + 1],
                                    scalar2=half_inv[bt][:, c:c + 1], op0=ALU.mult, op1=ALU.mult)

        def transpose_rows(i):
            u_ps[i] = ps_t.tile([P, PASSES, PAIRS, P], F32, name="u_ps")
            words = u_t[i][:].bitcast(F32)
            for g in range(PASSES):
                for e in range(PAIRS):
                    first = g * P * PAIRS + e
                    nc.tensor.transpose(u_ps[i][:, g, e, :],
                                        words[:, first:(g + 1) * P * PAIRS:PAIRS], ident[:])

        def regroup_rows(i):
            u_grp[i] = u_grouped.tile([P, PASSES, P, PAIRS], F32, name="u_grp", align_bytes=64)
            if i in VECTOR_REGROUPS:
                nc.vector.tensor_copy(out=u_grp[i][:], in_=u_ps[i][:].rearrange("p g e r -> p g r e"))
            else:
                nc.scalar.copy(out=u_grp[i][:], in_=u_ps[i][:].rearrange("p g e r -> p g r e"))

        def quantise_rows(i):
            nc.vector.quantize_mx(
                out=u_codes[:, i, :].bitcast(FP8X4),
                scales=u_scales[:, i, :],
                in_=u_grp[i][:].rearrange("p g r e -> p (g r e)").bitcast(BF16),
            )

        def multiply(i, h):
            y_ps[i, h] = ps_y.tile([P, BANK], F32, name="y_ps", tag="y_ps")
            for g in range(PASSES):
                nc.tensor.matmul_mx(
                    out=y_ps[i, h][:],
                    lhsT=u_codes[:, i, g * P:(g + 1) * P].bitcast(FP8X4),
                    lhsT_scale=u_scales[:, i, g * P:(g + 1) * P],
                    rhs=w_codes[:, g, h * BANK:(h + 1) * BANK].bitcast(FP8X4),
                    rhs_scale=w_scales[:, g, h * BANK:(h + 1) * BANK],
                    start=(g == 0),
                    stop=(g == PASSES - 1),
                )

        def add_bias(i, h):
            cols = slice(h * BANK, (h + 1) * BANK)
            nc.vector.tensor_tensor(out=y_all[:, i, cols], in0=y_ps[i, h][:], in1=b_all[:, cols], op=ALU.add)

        def scalar_relu(i, cols):
            y = y_all[:, i, cols]
            nc.scalar.activation(out=y, in_=y, func=ACT.Relu)

        def scalar_squares(i, cols, total):
            s_products = unread.tile([P, SIZE + EXTRA], F32, name="s_products")
            nc.scalar.activation(out=s_products[:, cols], in_=y_all[:, i, cols], func=ACT.Square, accum_out=total)

        def vector_squares(i, cols, total):
            y = y_all[:, i, cols]
            v_products = unread.tile([P, SIZE + EXTRA], F32, name="v_products")
            nc.vector.scalar_tensor_tensor(out=v_products[:, cols], in0=y, scalar=0.0, in1=y,
                                           op0=ALU.max, op1=ALU.mult, accum_out=total)

        def new_m_sq(i):
            m_sq[i] = stats.tile([P, 1], F32, name="m_sq")
            return m_sq[i][:]

        def norm2_root(i):
            inv_m[i] = stats.tile([P, 1], F32, name="inv_m")
            nc.gpsimd.tensor_tensor(out=inv_m[i][:], in0=m_sq[i][:], in1=minus_half[:, 0:1], op=ALU.pow)

        def out_tanh(i):
            tanh_m[i] = stats.tile([P, 1], F32, name="tanh_m")
            nc.scalar.activation(out=tanh_m[i][:], in_=m_sq[i][:], func=ACT.Tanh, scale=inv_m[i][:, 0:1])

        def out_gain(i):
            gain[i] = stats.tile([P, 1], F32, name="gain")
            nc.scalar.activation(out=gain[i][:], in_=tanh_m[i][:], func=ACT.Copy, scale=inv_m[i][:, 0:1])

        def scale_on_vector(i, cols):
            nc.vector.tensor_scalar(out=y_all[:, i, cols], in0=y_all[:, i, cols], scalar1=0.0,
                                    scalar2=gain[i][:, 0:1], op0=ALU.max, op1=ALU.mult)

        def scale_on_scalar(i, cols):
            nc.scalar.activation(out=y_all[:, i, cols], in_=y_all[:, i, cols], func=ACT.Relu,
                                 scale=gain[i][:, 0:1])

        def store(i, cols):
            nc.sync.dma_start(out=out_rows[:, i, cols], in_=y_all[:, i, cols])

        ctx.enter_context(tc.manual_schedule())
        nc.vector.memset(b_row[:].bitcast(U32), 0)
        nc.vector.memset(one[:], 1.0)
        nc.vector.memset(ones[:], 1.0)
        nc.gpsimd.memset(y_all[:, :, SIZE:SIZE + EXTRA], 1e-15)
        nc.gpsimd.memset(half[:], 0.5)
        nc.gpsimd.memset(minus_half[:], -0.5)
        make_identity(nc, ident[:])
        nc.scalar.activation(out=warm[:, 0:1], in_=one[:], func=ACT.Ln)
        load_rows(0, 2)
        nc.sync.dma_start(out=b_row[0:1, :], in_=b.rearrange("(o n) -> o n", o=1))
        load_w(0, (0,))
        load_rows(2, 2)
        load_w(1, (0,))
        load_rows(4, 2)
        load_w(0, (1,))
        load_w(1, (1,))
        load_rows(6, 2)

        square_sum(0)
        square_sum(1)
        norm_root(0)
        spread_ps()
        spread_copy()
        square_sum(2)
        regroup_w(0)
        norm_clip(0)
        log_terms(0)
        quantise_w(0)
        square_sum(3)
        norm_recip(0)
        regroup_w(1)
        log_ratios(0)
        square_sum(4)
        quantise_w(1)
        for i in (0, 1):
            scale_rows(i)
            transpose_rows(i)
        square_sum(5)
        norm_root(1)
        regroup_w(2)
        warm_tensor(2, 2)
        regroup_rows(0)
        regroup_rows(1)
        regroup_w(3)
        quantise_w(2)
        norm_clip(1)
        quantise_rows(0)
        multiply(0, 0)
        norm_recip(1)
        log_terms(1)
        quantise_rows(1)
        log_ratios(1)
        square_sum(6)
        quantise_w(3)
        multiply(0, 1)
        for i in (2, 3):
            scale_rows(i)
            transpose_rows(i)
        multiply(1, 0)
        multiply(1, 1)
        square_sum(7)
        norm_root(2)
        regroup_rows(2)
        regroup_rows(3)
        for i in (4, 5):
            scale_rows(i)
            transpose_rows(i)

        whole = slice(0, SIZE)
        summed = slice(0, SIZE + EXTRA)
        left, right = slice(0, BANK), slice(BANK, SIZE)
        add_bias(0, 0)
        add_bias(0, 1)
        scalar_relu(0, whole)
        add_bias(1, 0)
        add_bias(1, 1)
        norm_clip(2)
        quantise_rows(2)
        multiply(2, 0)
        multiply(2, 1)
        norm_recip(2)
        log_terms(2)
        regroup_rows(4)
        scalar_squares(0, summed, new_m_sq(0))
        nc.scalar.activation(out=warm[:, 1:2], in_=one[:], func=ACT.Tanh)
        quantise_rows(3)
        multiply(3, 0)
        multiply(3, 1)
        log_ratios(2)
        vector_squares(1, summed, new_m_sq(1))
        for i in (6, 7):
            scale_rows(i)
            transpose_rows(i)
        add_bias(2, 0)
        norm2_root(0)
        norm2_root(1)
        regroup_rows(5)
        add_bias(2, 1)
        add_bias(3, 0)
        quantise_rows(4)
        multiply(4, 0)
        multiply(4, 1)
        out_tanh(0)
        out_tanh(1)
        regroup_rows(6)
        out_gain(0)
        out_gain(1)
        scalar_relu(2, whole)
        scale_on_scalar(0, left)
        scalar_squares(2, summed, new_m_sq(2))
        scale_on_scalar(0, right)
        store(0, whole)
        regroup_rows(7)
        scale_on_scalar(1, left)
        add_bias(3, 1)
        quantise_rows(5)
        multiply(5, 0)
        multiply(5, 1)
        scale_on_scalar(1, right)
        store(1, whole)
        vector_squares(3, summed, new_m_sq(3))
        norm2_root(3)
        norm2_root(2)
        add_bias(4, 0)
        add_bias(4, 1)
        quantise_rows(6)
        multiply(6, 0)
        multiply(6, 1)
        vector_squares(4, summed, new_m_sq(4))
        norm2_root(4)
        add_bias(5, 0)
        add_bias(5, 1)
        quantise_rows(7)
        multiply(7, 0)
        multiply(7, 1)
        out_tanh(3)
        out_tanh(2)
        out_gain(3)
        out_gain(2)
        scale_on_scalar(2, whole)
        store(2, whole)
        scale_on_scalar(3, left)
        out_tanh(4)
        vector_squares(5, summed, new_m_sq(5))
        norm2_root(5)
        add_bias(6, 0)
        scale_on_scalar(3, right)
        store(3, whole)
        out_gain(4)
        add_bias(6, 1)
        add_bias(7, 0)
        scale_on_scalar(4, left)
        out_tanh(5)
        scale_on_scalar(4, right)
        store(4, whole)
        out_gain(5)
        vector_squares(6, summed, new_m_sq(6))
        norm2_root(6)
        add_bias(7, 1)
        scale_on_scalar(5, left)
        scale_on_vector(5, right)
        store(5, whole)
        out_tanh(6)
        out_gain(6)
        vector_squares(7, summed, new_m_sq(7))
        norm2_root(7)
        scale_on_scalar(6, left)
        scale_on_vector(6, right)
        store(6, whole)
        out_tanh(7)
        out_gain(7)
        scale_on_vector(7, slice(TAIL, SIZE))
        store(7, slice(TAIL, SIZE))
        scale_on_scalar(7, slice(0, TAIL))
        store(7, slice(0, TAIL))
